import numpy as np
import ml_dtypes


def mxq(x, axis, fmt="e4m3"):
    dtype, down = {"e4m3": (ml_dtypes.float8_e4m3fn, 7), "e5m2": (ml_dtypes.float8_e5m2, 14)}[fmt]
    v = np.moveaxis(np.asarray(x, np.float32).astype(ml_dtypes.bfloat16).astype(np.float64), axis, -1)
    blocks = v.reshape(v.shape[:-1] + (-1, 32))
    amax = np.abs(blocks).max(-1, keepdims=True)
    byte = np.maximum(np.where(amax > 0, np.frexp(amax)[1] - 1 + 127, 0) - down, 1)
    scale = np.exp2(byte - 127.0)
    codes = (blocks / scale).astype(np.float32).astype(dtype).astype(np.float64)
    return np.moveaxis((codes * scale).reshape(v.shape), -1, axis)


WIDE = False


def mx_kscale(k):
    if not WIDE:
        return np.ones(k)
    levels = np.array([10, -10, 5, -5, 0])
    if k % 512:
        return np.exp2(np.random.permutation(np.resize(levels, k // 32))).repeat(32)
    a = np.empty((k // 512, 16))
    for p in range(k // 512):
        a[p, :8] = np.random.permutation(np.resize(levels, 8))
        for g in range(8):
            far = levels[np.abs(levels - a[p, g]) >= 10]
            a[p, g + 8] = far[np.random.randint(len(far))]
    return np.exp2(a.ravel()).repeat(32)


BF16 = ml_dtypes.bfloat16


def bf(x):
    return np.asarray(x, np.float32).astype(BF16)


def f64(x):
    return np.asarray(x).astype(np.float64)


B, T, D, E, H, L = 128, 41, 1024, 128, 128, 1
TM = T - L
F = H + L * D + 1


def setup_inputs():
    s = mx_kscale(D)
    we = np.random.standard_normal((D, H)) / np.sqrt(H)
    wy = np.random.standard_normal((D, L, D)) * 0.7 / np.sqrt(L * D) / s
    wx = np.random.standard_normal((D, 1)) * 0.5 / s[:, None]
    return {"x": bf(np.random.standard_normal((B, T, D)) * s),
            "emb": bf(np.random.standard_normal((B, H)) * 0.5),
            "Wg": bf(np.concatenate([we, wy.reshape(D, L * D), wx], axis=1)),
            "bg": bf(np.random.standard_normal(D) * 0.3)}


def reference(x, emb, Wg, bg):
    xf = f64(x)
    Wy = f64(Wg)[:, H:H + L * D].reshape(D, L, D)
    wx = f64(Wg)[:, -1]
    ctx = f64(emb) @ f64(Wg)[:, :H].T
    xq = mxq(xf[:, :T - 1, :], 2, "e4m3")
    wq = mxq(Wy, 2, "e4m3")
    lag = sum((xq[:, l:TM + l, :] @ wq[:, l, :].T) for l in range(L))
    return ctx[:, None, :] + lag + xf[:, L:, :] * wx + f64(bg)

@@ -1,0 +1,211 @@
+from contextlib import ExitStack
+
+import concourse.mybir as mybir
+from concourse.masks import make_identity
+
+F32 = mybir.dt.float32
+BF16 = mybir.dt.bfloat16
+U32 = mybir.dt.uint32
+U8 = mybir.dt.uint8
+FP8X4 = mybir.dt.float8_e4m3fn_x4
+ADD = mybir.AluOpType.add
+MULT = mybir.AluOpType.mult
+
+P = 128
+STEPS = 41
+LAGS = STEPS - 1
+D = 1024
+ROW = P + D + 1
+ROW_PAD = 1168
+PASSES = 2
+WORD_BLOCKS = 4
+SLABS = 8
+CHUNK = 4
+N_CHUNKS = LAGS // CHUNK
+BANK = 512
+
+FLOPS = 2 * P * LAGS * D * D + 2 * P * P * D
+
+
+def word_block(first, w):
+    start = first + 2 * P * (w // 2) + w % 2
+    return slice(start, start + 2 * P - 1, 2)
+
+
+def regroup(copy, bank, grouped):
+    copy(out=grouped.bitcast(F32), in_=bank.rearrange("p (g u) c -> p g c u", u=2))
+
+
+def tile_npchangetransitionprior_pa_t_kernel(tc, x, emb, Wg, bg, out):
+    nc = tc.nc
+    with ExitStack() as ctx:
+        ctx.enter_context(tc.manual_schedule())
+        const = ctx.enter_context(tc.tile_pool(name="const", bufs=1))
+        xs_pool = ctx.enter_context(tc.tile_pool(name="xs_pool", bufs=3))
+        xg_pool = ctx.enter_context(tc.tile_pool(name="xg_pool", bufs=3))
+        xq_pool = ctx.enter_context(tc.tile_pool(name="xq_pool", bufs=2))
+        sum_pool = ctx.enter_context(tc.tile_pool(name="sum_pool", bufs=2))
+        res_pool = ctx.enter_context(tc.tile_pool(name="res_pool", bufs=6))
+        psum_in = ctx.enter_context(tc.psum_pool(name="psum_in", bufs=2))
+        psum_mx = ctx.enter_context(tc.psum_pool(name="psum_mx", bufs=3))
+        psum_back = ctx.enter_context(tc.psum_pool(name="psum_back", bufs=3))
+
+        x_rows = {}
+        x_grouped = {}
+        x_codes = {}
+        x_scales = {}
+        sums = {}
+
+        def load_chunk(c):
+            n_steps = min(CHUNK, STEPS - CHUNK * c)
+            rows = xs_pool.tile([P, CHUNK, D], BF16, name="rows")
+            nc.sync.dma_start(out=rows[:, 0:n_steps, :], in_=x[:, CHUNK * c : CHUNK * c + n_steps, :])
+            x_rows[c] = rows
+
+        load_chunk(0)
+        wg = const.tile([P, SLABS, ROW_PAD], BF16, name="wg")
+        wg_rows = Wg.rearrange("(g p t) c -> g p t c", p=P, t=4)
+        for w in range(WORD_BLOCKS):
+            t = 2 * (w % 2)
+            nc.sync.dma_start(out=wg[:, 2 * w : 2 * w + 2, 0:ROW], in_=wg_rows[w // 2, :, t : t + 2, :])
+        load_chunk(1)
+        load_chunk(2)
+        emb_rows = const.tile([P, P], BF16, name="emb_rows")
+        nc.scalar.dma_start(out=emb_rows[:], in_=emb)
+        bias_row = const.tile([P, D], BF16, name="bias_row")
+        nc.vector.memset(bias_row[:], 0.0)
+        nc.scalar.dma_start(out=bias_row[0:1, :], in_=bg.rearrange("(o d) -> o d", o=1))
+        ones = const.tile([P, P], BF16, name="ones")
+        nc.vector.memset(ones[:], 1.0)
+        ident_f32 = const.tile([P, P], F32, name="ident_f32")
+        make_identity(nc, ident_f32[:])
+        ident_bf16 = const.tile([P, P], BF16, name="ident_bf16")
+        make_identity(nc, ident_bf16[:])
+
+        def transpose_step(c, s):
+            words = x_rows[c][:].bitcast(F32)
+            bank = psum_in.tile([P, WORD_BLOCKS, P], F32, name="bank_in")
+            for w in range(WORD_BLOCKS):
+                nc.tensor.transpose(bank[:, w, :], words[:, s, word_block(0, w)], ident_f32[:])
+            if c < N_CHUNKS:
+                if s == 0:
+                    x_grouped[c] = xg_pool.tile([P, PASSES, CHUNK + 1, P, 4], BF16, name="grouped", align_bytes=64)
+                regroup(nc.scalar.copy, bank[:], x_grouped[c][:, :, s, :, :])
+            if s == 0 and c > 0:
+                regroup(nc.scalar.copy, bank[:], x_grouped[c - 1][:, :, CHUNK, :, :])
+
+        def quantise_pass(c, g):
+            if g == 0:
+                x_codes[c] = xq_pool.tile([P, PASSES, BANK], U32, name="codes", align_bytes=64)
+                x_scales[c] = xq_pool.tile([P, PASSES, BANK], U8, name="scales", align_bytes=64)
+            nc.vector.quantize_mx(
+                out=x_codes[c][:, g, :].bitcast(FP8X4),
+                scales=x_scales[c][:, g, :],
+                in_=x_grouped[c][:, g, 0:CHUNK, :, :].rearrange("p s b v -> p (s b v)"),
+            )
+
+        for s in range(CHUNK):
+            transpose_step(0, s)
+
+        wg_words = wg[:].bitcast(F32)
+        wy_word0 = P // 2
+        wy_grouped = const.tile([P, SLABS, PASSES, P, 4], BF16, name="wy_grouped", align_bytes=64)
+        wy_codes = const.tile([P, SLABS, PASSES, P], U32, name="wy_codes", align_bytes=64)
+        wy_scales = const.tile([P, SLABS, PASSES, P], U8, name="wy_scales", align_bytes=64)
+        for w in range(WORD_BLOCKS):
+            for e in range(2):
+                bank = psum_in.tile([P, WORD_BLOCKS, P], F32, name="bank_in")
+                for k in range(WORD_BLOCKS):
+                    nc.tensor.transpose(bank[:, k, :], wg_words[:, 2 * w + e, word_block(wy_word0, k)], ident_f32[:])
+                copy = nc.vector.tensor_copy if e == 0 else nc.scalar.copy
+                regroup(copy, bank[:], wy_grouped[:, 2 * w + e])
+            nc.vector.quantize_mx(
+                out=wy_codes[:, 2 * w : 2 * w + 2].rearrange("p l g m -> p (l g m)").bitcast(FP8X4),
+                scales=wy_scales[:, 2 * w : 2 * w + 2].rearrange("p l g m -> p (l g m)"),
+                in_=wy_grouped[:, 2 * w : 2 * w + 2].rearrange("p l g m v -> p (l g m v)"),
+            )
+        wx = const.tile([P, SLABS], F32, name="wx")
+        nc.vector.tensor_copy(out=wx[:].rearrange("p (w e) -> p w e", e=2), in_=wg[:, :, ROW - 1].rearrange("p (w e) -> p w e", e=2))
+
+        for s in range(CHUNK):
+            transpose_step(1, s)
+        for g in range(PASSES):
+            quantise_pass(0, g)
+
+        context = const.tile([P, D], F32, name="context")
+
+        def make_context():
+            emb_t_ps = psum_back.tile([P, P], BF16, name="emb_t_ps", tag="bank_back")
+            nc.tensor.transpose(emb_t_ps[:], emb_rows[:], ident_bf16[:])
+            emb_t = const.tile([P, P], BF16, name="emb_t")
+            nc.scalar.copy(out=emb_t[:], in_=emb_t_ps[:])
+            we_t_ps = psum_back.tile([P, SLABS, P], BF16, name="we_t_ps", tag="bank_back")
+            for slab in range(SLABS):
+                nc.tensor.transpose(we_t_ps[:, slab, :], wg[:, slab, 0:P], ident_bf16[:])
+            we_t = const.tile([P, D], BF16, name="we_t")
+            nc.scalar.copy(
+                out=we_t[:].rearrange("h (g p t) -> h g p t", p=P, t=4),
+                in_=we_t_ps[:].rearrange("h (g t) p -> h g p t", t=4),
+            )
+            for n in range(D // BANK):
+                cols = slice(BANK * n, BANK * (n + 1))
+                context_ps = psum_mx.tile([P, BANK], F32, name="context_ps", tag="product")
+                nc.tensor.matmul(context_ps[:], lhsT=emb_t[:], rhs=we_t[:, cols], start=True, stop=False)
+                nc.tensor.matmul(context_ps[:], lhsT=ones[:], rhs=bias_row[:, cols], start=False, stop=True)
+                nc.scalar.copy(out=context[:, cols], in_=context_ps[:])
+
+        def multiply_slab(c, slab):
+            product = psum_mx.tile([P, BANK], F32, name="product")
+            for g in range(PASSES):
+                nc.tensor.matmul_mx(
+                    out=product[:],
+                    lhsT=wy_codes[:, slab, g, :].bitcast(FP8X4),
+                    lhsT_scale=wy_scales[:, slab, g, :],
+                    rhs=x_codes[c][:, g, :].bitcast(FP8X4),
+                    rhs_scale=x_scales[c][:, g, :],
+                    start=(g == 0),
+                    stop=(g == PASSES - 1),
+                )
+            nc.vector.scalar_tensor_tensor(
+                out=sums[c][:, slab, :].rearrange("p (s b) -> p s b", s=CHUNK),
+                in0=x_grouped[c][:, slab // 4, 1 : CHUNK + 1, :, slab % 4],
+                scalar=wx[:, slab : slab + 1],
+                in1=product[:].rearrange("p (s b) -> p s b", s=CHUNK),
+                op0=MULT,
+                op1=ADD,
+            )
+
+        def finish_step(c, s):
+            res = res_pool.tile([P, D], F32, name="res")
+            for n in range(D // BANK):
+                cols = slice(BANK * n, BANK * (n + 1))
+                bank = psum_back.tile([P, 4, P], F32, name="bank_back")
+                for q in range(4):
+                    nc.tensor.transpose(bank[:, q, :], sums[c][:, 4 * n + q, P * s : P * (s + 1)], ident_f32[:])
+                in_order = bank[:].rearrange("b t p -> b p t")
+                res_half = res[:, cols].rearrange("b (p t) -> b p t", t=4)
+                if n == 0:
+                    context_half = context[:, cols].rearrange("b (p t) -> b p t", t=4)
+                    nc.vector.tensor_tensor(out=res_half, in0=in_order, in1=context_half, op=ADD)
+                else:
+                    nc.scalar.copy(out=res_half, in_=in_order)
+                    nc.gpsimd.tensor_tensor(out=res[:, cols], in0=res[:, cols], in1=context[:, cols], op=ADD)
+            nc.sync.dma_start(out=out[:, CHUNK * c + s, :], in_=res[:])
+
+        for i in range(N_CHUNKS + 1):
+            if CHUNK * (i + 3) < STEPS:
+                load_chunk(i + 3)
+            if i < N_CHUNKS:
+                sums[i] = sum_pool.tile([P, SLABS, BANK], F32, name="sums")
+            for k in range(CHUNK):
+                if i < N_CHUNKS:
+                    multiply_slab(i, 2 * k)
+                    multiply_slab(i, 2 * k + 1)
+                if i > 0:
+                    finish_step(i - 1, k)
+                if CHUNK * (i + 2) + k < STEPS:
+                    transpose_step(i + 2, k)
+                if k % 2 == 1 and i + 1 < N_CHUNKS:
+                    quantise_pass(i + 1, k // 2)
+            if i == 0:
+                make_context()

@@ -19,21 +19,36 @@ ROW = P + D + 1
 ROW_PAD = 1168
 PASSES = 2
 WORD_BLOCKS = 4
+WORDS = D // 2
 SLABS = 8
 CHUNK = 4
-N_CHUNKS = LAGS // CHUNK
 BANK = 512
+DIRECT = [2, 3, 3, 3, 3, 2]
+N_ROUNDS = len(DIRECT)
+SIZES = [CHUNK + n for n in DIRECT]
+STARTS = [sum(SIZES[:r]) for r in range(N_ROUNDS + 1)]
+SLOTS = max(SIZES)
+LEAD = 2
+FIRST_LEAD = 0
+MOST = 4
+AHEAD = 5
 
 FLOPS = 2 * P * LAGS * D * D + 2 * P * P * D
 
 
-def word_block(first, w):
-    start = first + 2 * P * (w // 2) + w % 2
-    return slice(start, start + 2 * P - 1, 2)
-
-
 def regroup(copy, bank, grouped):
     copy(out=grouped.bitcast(F32), in_=bank.rearrange("p (g u) c -> p g c u", u=2))
+
+
+def pieces(n):
+    out = []
+    first = 0
+    while n > 0:
+        size = 4 if n >= 4 else 2 if n >= 2 else 1
+        out.append((first, size))
+        first += size
+        n -= size
+    return out
 
 
 def tile_npchangetransitionprior_pa_t_kernel(tc, x, emb, Wg, bg, out):
@@ -41,98 +56,137 @@ def tile_npchangetransitionprior_pa_t_kernel(tc, x, emb, Wg, bg, out):
     with ExitStack() as ctx:
         ctx.enter_context(tc.manual_schedule())
         const = ctx.enter_context(tc.tile_pool(name="const", bufs=1))
-        xs_pool = ctx.enter_context(tc.tile_pool(name="xs_pool", bufs=3))
+        rows_pool = ctx.enter_context(tc.tile_pool(name="rows_pool", bufs=9))
+        perm_pool = ctx.enter_context(tc.tile_pool(name="perm_pool", bufs=4))
         xg_pool = ctx.enter_context(tc.tile_pool(name="xg_pool", bufs=3))
         xq_pool = ctx.enter_context(tc.tile_pool(name="xq_pool", bufs=2))
+        wyg_pool = ctx.enter_context(tc.tile_pool(name="wyg_pool", bufs=2))
         sum_pool = ctx.enter_context(tc.tile_pool(name="sum_pool", bufs=2))
-        res_pool = ctx.enter_context(tc.tile_pool(name="res_pool", bufs=6))
+        res_pool = ctx.enter_context(tc.tile_pool(name="res_pool", bufs=7))
+        y_pool = ctx.enter_context(tc.tile_pool(name="y_pool", bufs=7))
         psum_in = ctx.enter_context(tc.psum_pool(name="psum_in", bufs=2))
         psum_mx = ctx.enter_context(tc.psum_pool(name="psum_mx", bufs=3))
         psum_back = ctx.enter_context(tc.psum_pool(name="psum_back", bufs=3))
 
         x_rows = {}
+        x_perm = {}
         x_grouped = {}
-        x_codes = {}
-        x_scales = {}
+        chunk_codes = {}
+        chunk_scales = {}
+        direct_codes = {}
+        direct_scales = {}
         sums = {}
+        res = {}
+        y = {}
+        round_of = [r for r in range(N_ROUNDS) for _ in range(SIZES[r])]
 
-        def load_chunk(c):
-            n_steps = min(CHUNK, STEPS - CHUNK * c)
-            rows = xs_pool.tile([P, CHUNK, D], BF16, name="rows")
-            nc.sync.dma_start(out=rows[:, 0:n_steps, :], in_=x[:, CHUNK * c : CHUNK * c + n_steps, :])
-            x_rows[c] = rows
+        def load_steps(until):
+            while len(x_rows) <= min(until, STEPS - 1):
+                t = len(x_rows)
+                n = min(2, STEPS - t)
+                pair = rows_pool.tile([P, 2, D], BF16, name="rows")
+                nc.sync.dma_start(out=pair[:, 0:n, :], in_=x[:, t : t + n, :])
+                for s in range(n):
+                    x_rows[t + s] = pair[:, s, :]
 
-        load_chunk(0)
+        load_steps(CHUNK)
         wg = const.tile([P, SLABS, ROW_PAD], BF16, name="wg")
         wg_rows = Wg.rearrange("(g p t) c -> g p t c", p=P, t=4)
-        for w in range(WORD_BLOCKS):
+        for w in range(4):
             t = 2 * (w % 2)
             nc.sync.dma_start(out=wg[:, 2 * w : 2 * w + 2, 0:ROW], in_=wg_rows[w // 2, :, t : t + 2, :])
-        load_chunk(1)
-        load_chunk(2)
+        load_steps(13)
+        bias_row = const.tile([P, D], BF16, name="bias_row")
+        nc.gpsimd.memset(bias_row[:], 0.0)
         emb_rows = const.tile([P, P], BF16, name="emb_rows")
         nc.scalar.dma_start(out=emb_rows[:], in_=emb)
-        bias_row = const.tile([P, D], BF16, name="bias_row")
-        nc.vector.memset(bias_row[:], 0.0)
         nc.scalar.dma_start(out=bias_row[0:1, :], in_=bg.rearrange("(o d) -> o d", o=1))
-        ones = const.tile([P, P], BF16, name="ones")
-        nc.vector.memset(ones[:], 1.0)
         ident_f32 = const.tile([P, P], F32, name="ident_f32")
         make_identity(nc, ident_f32[:])
         ident_bf16 = const.tile([P, P], BF16, name="ident_bf16")
         make_identity(nc, ident_bf16[:])
+        ones = const.tile([P, P], BF16, name="ones")
+        nc.vector.memset(ones[:], 1.0)
 
-        def transpose_step(c, s):
-            words = x_rows[c][:].bitcast(F32)
+        def order_words(t, copy):
+            words = x_rows[t].bitcast(F32)
+            x_perm[t] = perm_pool.tile([P, PASSES, 2, P], F32, name="perm")
+            copy(out=x_perm[t][:], in_=words.rearrange("p (g m u) -> p g u m", g=PASSES, u=2))
+
+        def transpose_step(t, copy):
+            r = round_of[t]
+            slot = t - STARTS[r]
             bank = psum_in.tile([P, WORD_BLOCKS, P], F32, name="bank_in")
             for w in range(WORD_BLOCKS):
-                nc.tensor.transpose(bank[:, w, :], words[:, s, word_block(0, w)], ident_f32[:])
-            if c < N_CHUNKS:
-                if s == 0:
-                    x_grouped[c] = xg_pool.tile([P, PASSES, CHUNK + 1, P, 4], BF16, name="grouped", align_bytes=64)
-                regroup(nc.scalar.copy, bank[:], x_grouped[c][:, :, s, :, :])
-            if s == 0 and c > 0:
-                regroup(nc.scalar.copy, bank[:], x_grouped[c - 1][:, :, CHUNK, :, :])
+                if t in x_perm:
+                    block = x_perm[t][:, w // 2, w % 2, :]
+                else:
+                    first = 2 * P * (w // 2) + w % 2
+                    block = x_rows[t].bitcast(F32)[:, first : first + 2 * P - 1 : 2]
+                nc.tensor.transpose(bank[:, w, :], block, ident_f32[:])
+            if slot == 0:
+                x_grouped[r] = xg_pool.tile([P, PASSES, SLOTS, P, 4], BF16, name="grouped", align_bytes=64)
+            regroup(copy, bank[:], x_grouped[r][:, :, slot, :, :])
 
-        def quantise_pass(c, g):
+        def quantise_chunk(r, g):
             if g == 0:
-                x_codes[c] = xq_pool.tile([P, PASSES, BANK], U32, name="codes", align_bytes=64)
-                x_scales[c] = xq_pool.tile([P, PASSES, BANK], U8, name="scales", align_bytes=64)
+                chunk_codes[r] = xq_pool.tile([P, PASSES, BANK], U32, name="codes", align_bytes=64)
+                chunk_scales[r] = xq_pool.tile([P, PASSES, BANK], U8, name="scales", align_bytes=64)
             nc.vector.quantize_mx(
-                out=x_codes[c][:, g, :].bitcast(FP8X4),
-                scales=x_scales[c][:, g, :],
-                in_=x_grouped[c][:, g, 0:CHUNK, :, :].rearrange("p s b v -> p (s b v)"),
+                out=chunk_codes[r][:, g, :].bitcast(FP8X4),
+                scales=chunk_scales[r][:, g, :],
+                in_=x_grouped[r][:, g, 0:CHUNK, :, :].rearrange("p s b v -> p (s b v)"),
             )
 
-        for s in range(CHUNK):
-            transpose_step(0, s)
+        def quantise_direct(r, g):
+            n = DIRECT[r]
+            if g == 0:
+                direct_codes[r] = xq_pool.tile([P, PASSES, SLOTS - CHUNK, P], U32, name="dcodes", align_bytes=64)
+                direct_scales[r] = xq_pool.tile([P, PASSES, SLOTS - CHUNK, P], U8, name="dscales", align_bytes=64)
+            for first, size in pieces(n):
+                to = slice(first, first + size)
+                nc.vector.quantize_mx(
+                    out=direct_codes[r][:, g, to, :].rearrange("p s b -> p (s b)").bitcast(FP8X4),
+                    scales=direct_scales[r][:, g, to, :].rearrange("p s b -> p (s b)"),
+                    in_=x_grouped[r][:, g, CHUNK + first : CHUNK + first + size, :, :].rearrange("p s b v -> p (s b v)"),
+                )
 
         wg_words = wg[:].bitcast(F32)
-        wy_word0 = P // 2
-        wy_grouped = const.tile([P, SLABS, PASSES, P, 4], BF16, name="wy_grouped", align_bytes=64)
-        wy_codes = const.tile([P, SLABS, PASSES, P], U32, name="wy_codes", align_bytes=64)
-        wy_scales = const.tile([P, SLABS, PASSES, P], U8, name="wy_scales", align_bytes=64)
-        for w in range(WORD_BLOCKS):
+        wy_codes = const.tile([P, PASSES, SLABS, P], U32, name="wy_codes", align_bytes=64)
+        wy_scales = const.tile([P, PASSES, SLABS, P], U8, name="wy_scales", align_bytes=64)
+
+        def prepare_slabs(w):
+            grouped = wyg_pool.tile([P, PASSES, 2, P, 4], BF16, name="wy_grouped", align_bytes=64)
             for e in range(2):
                 bank = psum_in.tile([P, WORD_BLOCKS, P], F32, name="bank_in")
                 for k in range(WORD_BLOCKS):
-                    nc.tensor.transpose(bank[:, k, :], wg_words[:, 2 * w + e, word_block(wy_word0, k)], ident_f32[:])
+                    first = P // 2 + 2 * P * (k // 2) + k % 2
+                    nc.tensor.transpose(
+                        bank[:, k, :], wg_words[:, 2 * w + e, first : first + 2 * P - 1 : 2], ident_f32[:]
+                    )
                 copy = nc.vector.tensor_copy if e == 0 else nc.scalar.copy
-                regroup(copy, bank[:], wy_grouped[:, 2 * w + e])
-            nc.vector.quantize_mx(
-                out=wy_codes[:, 2 * w : 2 * w + 2].rearrange("p l g m -> p (l g m)").bitcast(FP8X4),
-                scales=wy_scales[:, 2 * w : 2 * w + 2].rearrange("p l g m -> p (l g m)"),
-                in_=wy_grouped[:, 2 * w : 2 * w + 2].rearrange("p l g m v -> p (l g m v)"),
-            )
+                regroup(copy, bank[:], grouped[:, :, e, :, :])
+            for g in range(PASSES):
+                nc.vector.quantize_mx(
+                    out=wy_codes[:, g, 2 * w : 2 * w + 2, :].rearrange("p l m -> p (l m)").bitcast(FP8X4),
+                    scales=wy_scales[:, g, 2 * w : 2 * w + 2, :].rearrange("p l m -> p (l m)"),
+                    in_=grouped[:, g, :, :, :].rearrange("p l m v -> p (l m v)"),
+                )
+
         wx = const.tile([P, SLABS], F32, name="wx")
-        nc.vector.tensor_copy(out=wx[:].rearrange("p (w e) -> p w e", e=2), in_=wg[:, :, ROW - 1].rearrange("p (w e) -> p w e", e=2))
-
-        for s in range(CHUNK):
-            transpose_step(1, s)
-        for g in range(PASSES):
-            quantise_pass(0, g)
-
+        wx_all = const.tile([P, D], F32, name="wx_all")
         context = const.tile([P, D], F32, name="context")
+
+        def make_wx():
+            for g in range(PASSES):
+                bank = psum_back.tile([P, 4, P], F32, name="wx_ps", tag="bank_back")
+                for t in range(4):
+                    slab = 4 * g + t
+                    nc.tensor.transpose(bank[:, t, :], wx[:, slab : slab + 1].to_broadcast([P, P]), ident_f32[:])
+                nc.scalar.copy(
+                    out=wx_all[:, BANK * g : BANK * (g + 1)].rearrange("b (p t) -> b p t", t=4),
+                    in_=bank[:].rearrange("b t p -> b p t"),
+                )
 
         def make_context():
             emb_t_ps = psum_back.tile([P, P], BF16, name="emb_t_ps", tag="bank_back")
@@ -143,69 +197,141 @@ def tile_npchangetransitionprior_pa_t_kernel(tc, x, emb, Wg, bg, out):
             for slab in range(SLABS):
                 nc.tensor.transpose(we_t_ps[:, slab, :], wg[:, slab, 0:P], ident_bf16[:])
             we_t = const.tile([P, D], BF16, name="we_t")
-            nc.scalar.copy(
+            nc.vector.tensor_copy(
                 out=we_t[:].rearrange("h (g p t) -> h g p t", p=P, t=4),
                 in_=we_t_ps[:].rearrange("h (g t) p -> h g p t", t=4),
             )
             for n in range(D // BANK):
                 cols = slice(BANK * n, BANK * (n + 1))
-                context_ps = psum_mx.tile([P, BANK], F32, name="context_ps", tag="product")
+                context_ps = psum_back.tile([P, BANK], F32, name="context_ps", tag="bank_back")
                 nc.tensor.matmul(context_ps[:], lhsT=emb_t[:], rhs=we_t[:, cols], start=True, stop=False)
                 nc.tensor.matmul(context_ps[:], lhsT=ones[:], rhs=bias_row[:, cols], start=False, stop=True)
-                nc.scalar.copy(out=context[:, cols], in_=context_ps[:])
+                copy = nc.vector.tensor_copy if n == 0 else nc.scalar.copy
+                copy(out=context[:, cols], in_=context_ps[:])
 
-        def multiply_slab(c, slab):
+        def multiply_slab(r, slab):
+            if slab % 4 == 0:
+                sums[r, slab // 4] = sum_pool.tile([P, 4, BANK], F32, name="sums")
             product = psum_mx.tile([P, BANK], F32, name="product")
             for g in range(PASSES):
                 nc.tensor.matmul_mx(
                     out=product[:],
-                    lhsT=wy_codes[:, slab, g, :].bitcast(FP8X4),
-                    lhsT_scale=wy_scales[:, slab, g, :],
-                    rhs=x_codes[c][:, g, :].bitcast(FP8X4),
-                    rhs_scale=x_scales[c][:, g, :],
+                    lhsT=wy_codes[:, g, slab, :].bitcast(FP8X4),
+                    lhsT_scale=wy_scales[:, g, slab, :],
+                    rhs=chunk_codes[r][:, g, :].bitcast(FP8X4),
+                    rhs_scale=chunk_scales[r][:, g, :],
                     start=(g == 0),
                     stop=(g == PASSES - 1),
                 )
             nc.vector.scalar_tensor_tensor(
-                out=sums[c][:, slab, :].rearrange("p (s b) -> p s b", s=CHUNK),
-                in0=x_grouped[c][:, slab // 4, 1 : CHUNK + 1, :, slab % 4],
+                out=sums[r, slab // 4][:, slab % 4, :].rearrange("p (s b) -> p s b", s=CHUNK),
+                in0=x_grouped[r][:, slab // 4, 1 : CHUNK + 1, :, slab % 4],
                 scalar=wx[:, slab : slab + 1],
                 in1=product[:].rearrange("p (s b) -> p s b", s=CHUNK),
                 op0=MULT,
                 op1=ADD,
             )
 
-        def finish_step(c, s):
-            res = res_pool.tile([P, D], F32, name="res")
-            for n in range(D // BANK):
-                cols = slice(BANK * n, BANK * (n + 1))
-                bank = psum_back.tile([P, 4, P], F32, name="bank_back")
-                for q in range(4):
-                    nc.tensor.transpose(bank[:, q, :], sums[c][:, 4 * n + q, P * s : P * (s + 1)], ident_f32[:])
-                in_order = bank[:].rearrange("b t p -> b p t")
-                res_half = res[:, cols].rearrange("b (p t) -> b p t", t=4)
-                if n == 0:
-                    context_half = context[:, cols].rearrange("b (p t) -> b p t", t=4)
-                    nc.vector.tensor_tensor(out=res_half, in0=in_order, in1=context_half, op=ADD)
-                else:
-                    nc.scalar.copy(out=res_half, in_=in_order)
-                    nc.gpsimd.tensor_tensor(out=res[:, cols], in0=res[:, cols], in1=context[:, cols], op=ADD)
-            nc.sync.dma_start(out=out[:, CHUNK * c + s, :], in_=res[:])
+        def start_direct(r, i):
+            t = STARTS[r] + CHUNK + i
+            y[t] = y_pool.tile([P, D], F32, name="y")
+            nc.gpsimd.tensor_tensor(out=y[t][:], in0=x_rows[t + 1], in1=wx_all[:], op=MULT)
+            nc.gpsimd.tensor_tensor(out=y[t][:], in0=y[t][:], in1=context[:], op=ADD)
 
-        for i in range(N_CHUNKS + 1):
-            if CHUNK * (i + 3) < STEPS:
-                load_chunk(i + 3)
-            if i < N_CHUNKS:
-                sums[i] = sum_pool.tile([P, SLABS, BANK], F32, name="sums")
-            for k in range(CHUNK):
-                if i < N_CHUNKS:
-                    multiply_slab(i, 2 * k)
-                    multiply_slab(i, 2 * k + 1)
-                if i > 0:
-                    finish_step(i - 1, k)
-                if CHUNK * (i + 2) + k < STEPS:
-                    transpose_step(i + 2, k)
-                if k % 2 == 1 and i + 1 < N_CHUNKS:
-                    quantise_pass(i + 1, k // 2)
-            if i == 0:
+        def multiply_direct(r, i, n):
+            t = STARTS[r] + CHUNK + i
+            product = psum_mx.tile([P, BANK], F32, name="product")
+            for g in range(PASSES):
+                nc.tensor.matmul_mx(
+                    out=product[:],
+                    lhsT=direct_codes[r][:, g, i, :].bitcast(FP8X4),
+                    lhsT_scale=direct_scales[r][:, g, i, :],
+                    rhs=wy_codes[:, g, 4 * n : 4 * n + 4, :].rearrange("p l m -> p (l m)").bitcast(FP8X4),
+                    rhs_scale=wy_scales[:, g, 4 * n : 4 * n + 4, :].rearrange("p l m -> p (l m)"),
+                    start=(g == 0),
+                    stop=(g == PASSES - 1),
+                )
+            half = y[t][:, BANK * n : BANK * (n + 1)].rearrange("b (p t) -> b p t", t=4)
+            nc.vector.tensor_tensor(
+                out=half, in0=product[:].rearrange("b (t p) -> b p t", t=4), in1=half, op=ADD
+            )
+            if n == 1:
+                nc.sync.dma_start(out=out[:, t, :], in_=y[t][:])
+
+        def finish_half(r, n, s):
+            if n == 0:
+                res[r, s] = res_pool.tile([P, D], F32, name="res")
+            cols = slice(BANK * n, BANK * (n + 1))
+            bank = psum_back.tile([P, 4, P], F32, name="bank_back")
+            for q in range(4):
+                nc.tensor.transpose(bank[:, q, :], sums[r, n][:, q, P * s : P * (s + 1)], ident_f32[:])
+            nc.vector.tensor_tensor(
+                out=res[r, s][:, cols].rearrange("b (p t) -> b p t", t=4),
+                in0=bank[:].rearrange("b t p -> b p t"),
+                in1=context[:, cols].rearrange("b (p t) -> b p t", t=4),
+                op=ADD,
+            )
+            if n == 1:
+                nc.sync.dma_start(out=out[:, STARTS[r] + s, :], in_=res[r, s][:])
+
+        for t in range(CHUNK + 1):
+            transpose_step(t, nc.scalar.copy if t % 2 == 0 else nc.vector.tensor_copy)
+        for g in range(PASSES):
+            quantise_chunk(0, g)
+        prepare_slabs(0)
+        prepare_slabs(1)
+        nc.scalar.copy(out=wx[:], in_=wg[:, :, ROW - 1])
+        done = CHUNK + 1
+
+        def direct_halves(q):
+            r = (q - 2) // CHUNK
+            k = (q - 2) % CHUNK
+            if r < 0 or r >= N_ROUNDS:
+                return []
+            halves = [(r, j, n) for j in range(DIRECT[r]) for n in range(2)]
+            return halves[len(halves) * k // CHUNK : len(halves) * (k + 1) // CHUNK]
+
+        for q in range(CHUNK * N_ROUNDS + 2):
+            i = q // CHUNK
+            k = q % CHUNK
+            steps = []
+            if i + 1 < N_ROUNDS:
+                lead = min(LEAD, FIRST_LEAD + q // 2)
+                goal = min(LAGS, STARTS[i + 1] + -(-SIZES[i + 1] * (k + 1) // CHUNK) + lead)
+                steps = list(range(done, min(goal, done + MOST)))
+            elif done < LAGS:
+                steps = list(range(done, min(LAGS, done + MOST)))
+            done += len(steps)
+            load_steps(done + AHEAD)
+            if k == 2 and i + 1 < N_ROUNDS:
+                for j in range(DIRECT[i + 1]):
+                    start_direct(i + 1, j)
+            if i > 0:
+                for t in steps:
+                    order_words(t, nc.scalar.copy)
+            if i < N_ROUNDS:
+                multiply_slab(i, 2 * k)
+                multiply_slab(i, 2 * k + 1)
+            if 0 < i < N_ROUNDS and k < 2:
+                quantise_direct(i, k)
+            if i + 1 < N_ROUNDS and k >= 2:
+                quantise_chunk(i + 1, k - 2)
+            for r, j, n in direct_halves(q):
+                multiply_direct(r, j, n)
+            if q < 2:
+                prepare_slabs(q + 2)
+            if q == 0:
+                make_wx()
                 make_context()
+                for j in range(DIRECT[0]):
+                    start_direct(0, j)
+            if q >= 2:
+                r = (q - 2) // CHUNK
+                n = k // 2 ^ 1
+                for s in range(2 * (k % 2), 2 * (k % 2) + 2):
+                    finish_half(r, n, s)
+            for t in steps:
+                transpose_step(t, nc.vector.tensor_copy if i == 0 and t % 2 == 1 else nc.scalar.copy)
+            if q == 1:
+                for g in range(PASSES):
+                    quantise_direct(0, g)

@@ -19,19 +19,20 @@ ROW = P + D + 1
 ROW_PAD = 1168
 PASSES = 2
 WORD_BLOCKS = 4
-WORDS = D // 2
 SLABS = 8
 CHUNK = 4
 BANK = 512
-DIRECT = [2, 3, 3, 3, 3, 2]
-N_ROUNDS = len(DIRECT)
-SIZES = [CHUNK + n for n in DIRECT]
-STARTS = [sum(SIZES[:r]) for r in range(N_ROUNDS + 1)]
-SLOTS = max(SIZES)
-LEAD = 2
-FIRST_LEAD = 0
-MOST = 4
+GROUPS = [("C", 4), ("C", 4), ("B", 4), ("C", 8), ("B", 4), ("C", 8), ("B", 4), ("B", 4)]
+FIRST = [sum(n for _, n in GROUPS[:i]) for i in range(len(GROUPS))]
+GROUP_OF = [i for i, (_, n) in enumerate(GROUPS) for _ in range(n)]
+CHUNKS = [FIRST[i] + CHUNK * c for i, (kind, n) in enumerate(GROUPS) if kind == "C" for c in range(n // CHUNK)]
+DIRECT = [t for t in range(LAGS) if GROUPS[GROUP_OF[t]][0] == "B"]
+QUARTERS = CHUNK * len(CHUNKS)
+G_COLS = 256
 AHEAD = 5
+B_FROM = 5
+B_TO = QUARTERS + 2
+WARM = 8
 
 FLOPS = 2 * P * LAGS * D * D + 2 * P * P * D
 
@@ -40,45 +41,30 @@ def regroup(copy, bank, grouped):
     copy(out=grouped.bitcast(F32), in_=bank.rearrange("p (g u) c -> p g c u", u=2))
 
 
-def pieces(n):
-    out = []
-    first = 0
-    while n > 0:
-        size = 4 if n >= 4 else 2 if n >= 2 else 1
-        out.append((first, size))
-        first += size
-        n -= size
-    return out
-
-
 def tile_npchangetransitionprior_pa_t_kernel(tc, x, emb, Wg, bg, out):
     nc = tc.nc
     with ExitStack() as ctx:
         ctx.enter_context(tc.manual_schedule())
         const = ctx.enter_context(tc.tile_pool(name="const", bufs=1))
         rows_pool = ctx.enter_context(tc.tile_pool(name="rows_pool", bufs=9))
-        perm_pool = ctx.enter_context(tc.tile_pool(name="perm_pool", bufs=4))
-        xg_pool = ctx.enter_context(tc.tile_pool(name="xg_pool", bufs=3))
+        perm_pool = ctx.enter_context(tc.tile_pool(name="perm_pool", bufs=5))
+        xg_pool = ctx.enter_context(tc.tile_pool(name="xg_pool", bufs=2))
         xq_pool = ctx.enter_context(tc.tile_pool(name="xq_pool", bufs=2))
         wyg_pool = ctx.enter_context(tc.tile_pool(name="wyg_pool", bufs=2))
         sum_pool = ctx.enter_context(tc.tile_pool(name="sum_pool", bufs=2))
-        res_pool = ctx.enter_context(tc.tile_pool(name="res_pool", bufs=7))
-        y_pool = ctx.enter_context(tc.tile_pool(name="y_pool", bufs=7))
+        res_pool = ctx.enter_context(tc.tile_pool(name="res_pool", bufs=3))
+        y_pool = ctx.enter_context(tc.tile_pool(name="y_pool", bufs=6))
         psum_in = ctx.enter_context(tc.psum_pool(name="psum_in", bufs=2))
         psum_mx = ctx.enter_context(tc.psum_pool(name="psum_mx", bufs=3))
         psum_back = ctx.enter_context(tc.psum_pool(name="psum_back", bufs=3))
 
         x_rows = {}
         x_perm = {}
-        x_grouped = {}
-        chunk_codes = {}
-        chunk_scales = {}
-        direct_codes = {}
-        direct_scales = {}
+        grouped = {}
+        codes = {}
+        scales = {}
         sums = {}
-        res = {}
         y = {}
-        round_of = [r for r in range(N_ROUNDS) for _ in range(SIZES[r])]
 
         def load_steps(until):
             while len(x_rows) <= min(until, STEPS - 1):
@@ -89,88 +75,88 @@ def tile_npchangetransitionprior_pa_t_kernel(tc, x, emb, Wg, bg, out):
                 for s in range(n):
                     x_rows[t + s] = pair[:, s, :]
 
-        load_steps(CHUNK)
+        emb_rows = const.tile([P, P], BF16, name="emb_rows")
+        nc.sync.dma_start(out=emb_rows[:], in_=emb)
+        load_steps(3)
         wg = const.tile([P, SLABS, ROW_PAD], BF16, name="wg")
         wg_rows = Wg.rearrange("(g p t) c -> g p t c", p=P, t=4)
         for w in range(4):
             t = 2 * (w % 2)
             nc.sync.dma_start(out=wg[:, 2 * w : 2 * w + 2, 0:ROW], in_=wg_rows[w // 2, :, t : t + 2, :])
-        load_steps(13)
+            if w == 0:
+                load_steps(4)
+        load_steps(11)
+        ones = const.tile([P, P], BF16, name="ones")
+        nc.vector.memset(ones[:], 1.0)
         bias_row = const.tile([P, D], BF16, name="bias_row")
-        nc.gpsimd.memset(bias_row[:], 0.0)
-        emb_rows = const.tile([P, P], BF16, name="emb_rows")
-        nc.scalar.dma_start(out=emb_rows[:], in_=emb)
+        nc.vector.memset(bias_row[:], 0.0)
+        for i in range(WARM):
+            warm = psum_mx.tile([P, BANK], F32, name="warm", tag="product")
+            nc.tensor.matmul(warm[:], lhsT=ones[:], rhs=bias_row[:, 0:BANK], start=True, stop=True)
         nc.scalar.dma_start(out=bias_row[0:1, :], in_=bg.rearrange("(o d) -> o d", o=1))
         ident_f32 = const.tile([P, P], F32, name="ident_f32")
         make_identity(nc, ident_f32[:])
         ident_bf16 = const.tile([P, P], BF16, name="ident_bf16")
         make_identity(nc, ident_bf16[:])
-        ones = const.tile([P, P], BF16, name="ones")
-        nc.vector.memset(ones[:], 1.0)
 
-        def order_words(t, copy):
-            words = x_rows[t].bitcast(F32)
-            x_perm[t] = perm_pool.tile([P, PASSES, 2, P], F32, name="perm")
-            copy(out=x_perm[t][:], in_=words.rearrange("p (g m u) -> p g u m", g=PASSES, u=2))
+        def order_words(copy, words):
+            perm = perm_pool.tile([P, PASSES, 2, P], F32, name="perm")
+            copy(out=perm[:], in_=words.rearrange("p (g m u) -> p g u m", g=PASSES, u=2))
+            return perm
 
-        def transpose_step(t, copy):
-            r = round_of[t]
-            slot = t - STARTS[r]
+        def transpose_words(perm):
             bank = psum_in.tile([P, WORD_BLOCKS, P], F32, name="bank_in")
             for w in range(WORD_BLOCKS):
-                if t in x_perm:
-                    block = x_perm[t][:, w // 2, w % 2, :]
-                else:
-                    first = 2 * P * (w // 2) + w % 2
-                    block = x_rows[t].bitcast(F32)[:, first : first + 2 * P - 1 : 2]
-                nc.tensor.transpose(bank[:, w, :], block, ident_f32[:])
-            if slot == 0:
-                x_grouped[r] = xg_pool.tile([P, PASSES, SLOTS, P, 4], BF16, name="grouped", align_bytes=64)
-            regroup(copy, bank[:], x_grouped[r][:, :, slot, :, :])
+                nc.tensor.transpose(bank[:, w, :], perm[:, w // 2, w % 2, :], ident_f32[:])
+            return bank
 
-        def quantise_chunk(r, g):
-            if g == 0:
-                chunk_codes[r] = xq_pool.tile([P, PASSES, BANK], U32, name="codes", align_bytes=64)
-                chunk_scales[r] = xq_pool.tile([P, PASSES, BANK], U8, name="scales", align_bytes=64)
-            nc.vector.quantize_mx(
-                out=chunk_codes[r][:, g, :].bitcast(FP8X4),
-                scales=chunk_scales[r][:, g, :],
-                in_=x_grouped[r][:, g, 0:CHUNK, :, :].rearrange("p s b v -> p (s b v)"),
-            )
-
-        def quantise_direct(r, g):
-            n = DIRECT[r]
-            if g == 0:
-                direct_codes[r] = xq_pool.tile([P, PASSES, SLOTS - CHUNK, P], U32, name="dcodes", align_bytes=64)
-                direct_scales[r] = xq_pool.tile([P, PASSES, SLOTS - CHUNK, P], U8, name="dscales", align_bytes=64)
-            for first, size in pieces(n):
-                to = slice(first, first + size)
-                nc.vector.quantize_mx(
-                    out=direct_codes[r][:, g, to, :].rearrange("p s b -> p (s b)").bitcast(FP8X4),
-                    scales=direct_scales[r][:, g, to, :].rearrange("p s b -> p (s b)"),
-                    in_=x_grouped[r][:, g, CHUNK + first : CHUNK + first + size, :, :].rearrange("p s b v -> p (s b v)"),
+        def place_step(t, bank, copy):
+            i = GROUP_OF[t]
+            kind, n = GROUPS[i]
+            if t == FIRST[i]:
+                slots = n + 1 if kind == "C" else n
+                grouped[i] = xg_pool.tile(
+                    [P, PASSES, slots, P, 4], BF16, name="grouped", tag="grouped_" + kind, align_bytes=64
                 )
+                if i > 0 and GROUPS[i - 1][0] == "C":
+                    regroup(copy, bank[:], grouped[i - 1][:, :, GROUPS[i - 1][1], :, :])
+            regroup(copy, bank[:], grouped[i][:, :, t - FIRST[i], :, :])
+
+        def quantise(i, g):
+            kind, n = GROUPS[i]
+            if g == 0:
+                codes[i] = xq_pool.tile([P, PASSES, n * P], U32, name="codes", tag="codes_" + kind, align_bytes=64)
+                scales[i] = xq_pool.tile([P, PASSES, n * P], U8, name="scales", tag="scales_" + kind, align_bytes=64)
+            nc.vector.quantize_mx(
+                out=codes[i][:, g, :].bitcast(FP8X4),
+                scales=scales[i][:, g, :],
+                in_=grouped[i][:, g, 0:n, :, :].rearrange("p s b v -> p (s b v)"),
+            )
 
         wg_words = wg[:].bitcast(F32)
         wy_codes = const.tile([P, PASSES, SLABS, P], U32, name="wy_codes", align_bytes=64)
         wy_scales = const.tile([P, PASSES, SLABS, P], U8, name="wy_scales", align_bytes=64)
+        wy_perm = {}
+        wy_grouped = {}
 
-        def prepare_slabs(w):
-            grouped = wyg_pool.tile([P, PASSES, 2, P, 4], BF16, name="wy_grouped", align_bytes=64)
+        def order_slabs(w):
             for e in range(2):
-                bank = psum_in.tile([P, WORD_BLOCKS, P], F32, name="bank_in")
-                for k in range(WORD_BLOCKS):
-                    first = P // 2 + 2 * P * (k // 2) + k % 2
-                    nc.tensor.transpose(
-                        bank[:, k, :], wg_words[:, 2 * w + e, first : first + 2 * P - 1 : 2], ident_f32[:]
-                    )
-                copy = nc.vector.tensor_copy if e == 0 else nc.scalar.copy
-                regroup(copy, bank[:], grouped[:, :, e, :, :])
+                words = wg_words[:, 2 * w + e, P // 2 : P // 2 + D // 2]
+                wy_perm[2 * w + e] = order_words(nc.vector.tensor_copy, words)
+
+        def turn_slabs(w):
+            wy_grouped[w] = wyg_pool.tile([P, PASSES, 2, P, 4], BF16, name="wy_grouped", align_bytes=64)
+            for e in range(2):
+                bank = transpose_words(wy_perm[2 * w + e])
+                copy = nc.vector.tensor_copy if e == 1 and w > 0 else nc.scalar.copy
+                regroup(copy, bank[:], wy_grouped[w][:, :, e, :, :])
+
+        def quantise_slabs(w):
             for g in range(PASSES):
                 nc.vector.quantize_mx(
                     out=wy_codes[:, g, 2 * w : 2 * w + 2, :].rearrange("p l m -> p (l m)").bitcast(FP8X4),
                     scales=wy_scales[:, g, 2 * w : 2 * w + 2, :].rearrange("p l m -> p (l m)"),
-                    in_=grouped[:, g, :, :, :].rearrange("p l m v -> p (l m v)"),
+                    in_=wy_grouped[w][:, g, :, :, :].rearrange("p l m v -> p (l m v)"),
                 )
 
         wx = const.tile([P, SLABS], F32, name="wx")
@@ -188,150 +174,152 @@ def tile_npchangetransitionprior_pa_t_kernel(tc, x, emb, Wg, bg, out):
                     in_=bank[:].rearrange("b t p -> b p t"),
                 )
 
-        def make_context():
+        emb_t = const.tile([P, P], BF16, name="emb_t")
+        we_t = const.tile([P, D], BF16, name="we_t")
+
+        def turn_context():
             emb_t_ps = psum_back.tile([P, P], BF16, name="emb_t_ps", tag="bank_back")
             nc.tensor.transpose(emb_t_ps[:], emb_rows[:], ident_bf16[:])
-            emb_t = const.tile([P, P], BF16, name="emb_t")
             nc.scalar.copy(out=emb_t[:], in_=emb_t_ps[:])
             we_t_ps = psum_back.tile([P, SLABS, P], BF16, name="we_t_ps", tag="bank_back")
             for slab in range(SLABS):
                 nc.tensor.transpose(we_t_ps[:, slab, :], wg[:, slab, 0:P], ident_bf16[:])
-            we_t = const.tile([P, D], BF16, name="we_t")
             nc.vector.tensor_copy(
                 out=we_t[:].rearrange("h (g p t) -> h g p t", p=P, t=4),
                 in_=we_t_ps[:].rearrange("h (g t) p -> h g p t", t=4),
             )
+
+        def make_context():
             for n in range(D // BANK):
                 cols = slice(BANK * n, BANK * (n + 1))
                 context_ps = psum_back.tile([P, BANK], F32, name="context_ps", tag="bank_back")
                 nc.tensor.matmul(context_ps[:], lhsT=emb_t[:], rhs=we_t[:, cols], start=True, stop=False)
                 nc.tensor.matmul(context_ps[:], lhsT=ones[:], rhs=bias_row[:, cols], start=False, stop=True)
-                copy = nc.vector.tensor_copy if n == 0 else nc.scalar.copy
-                copy(out=context[:, cols], in_=context_ps[:])
+                nc.vector.tensor_copy(out=context[:, cols], in_=context_ps[:])
 
-        def multiply_slab(r, slab):
+        def multiply_slab(c, slab):
+            i = GROUP_OF[CHUNKS[c]]
+            s0 = CHUNKS[c] - FIRST[i]
+            cols = slice(P * s0, P * (s0 + CHUNK))
             if slab % 4 == 0:
-                sums[r, slab // 4] = sum_pool.tile([P, 4, BANK], F32, name="sums")
+                sums[c, slab // 4] = sum_pool.tile([P, 4, BANK], F32, name="sums")
             product = psum_mx.tile([P, BANK], F32, name="product")
             for g in range(PASSES):
                 nc.tensor.matmul_mx(
                     out=product[:],
                     lhsT=wy_codes[:, g, slab, :].bitcast(FP8X4),
                     lhsT_scale=wy_scales[:, g, slab, :],
-                    rhs=chunk_codes[r][:, g, :].bitcast(FP8X4),
-                    rhs_scale=chunk_scales[r][:, g, :],
+                    rhs=codes[i][:, g, cols].bitcast(FP8X4),
+                    rhs_scale=scales[i][:, g, cols],
                     start=(g == 0),
                     stop=(g == PASSES - 1),
                 )
             nc.vector.scalar_tensor_tensor(
-                out=sums[r, slab // 4][:, slab % 4, :].rearrange("p (s b) -> p s b", s=CHUNK),
-                in0=x_grouped[r][:, slab // 4, 1 : CHUNK + 1, :, slab % 4],
+                out=sums[c, slab // 4][:, slab % 4, :].rearrange("p (s b) -> p s b", s=CHUNK),
+                in0=grouped[i][:, slab // 4, s0 + 1 : s0 + 1 + CHUNK, :, slab % 4],
                 scalar=wx[:, slab : slab + 1],
                 in1=product[:].rearrange("p (s b) -> p s b", s=CHUNK),
                 op0=MULT,
                 op1=ADD,
             )
 
-        def start_direct(r, i):
-            t = STARTS[r] + CHUNK + i
+        def start_direct(t):
             y[t] = y_pool.tile([P, D], F32, name="y")
-            nc.gpsimd.tensor_tensor(out=y[t][:], in0=x_rows[t + 1], in1=wx_all[:], op=MULT)
-            nc.gpsimd.tensor_tensor(out=y[t][:], in0=y[t][:], in1=context[:], op=ADD)
+            for c in range(0, D, G_COLS):
+                cols = slice(c, c + G_COLS)
+                nc.gpsimd.tensor_tensor(out=y[t][:, cols], in0=x_rows[t + 1][:, cols], in1=wx_all[:, cols], op=MULT)
+            for c in range(0, D, G_COLS):
+                cols = slice(c, c + G_COLS)
+                nc.gpsimd.tensor_tensor(out=y[t][:, cols], in0=y[t][:, cols], in1=context[:, cols], op=ADD)
 
-        def multiply_direct(r, i, n):
-            t = STARTS[r] + CHUNK + i
+        def multiply_direct(t, n):
+            i = GROUP_OF[t]
+            rows = slice(P * (t - FIRST[i]), P * (t - FIRST[i] + 1))
             product = psum_mx.tile([P, BANK], F32, name="product")
             for g in range(PASSES):
                 nc.tensor.matmul_mx(
                     out=product[:],
-                    lhsT=direct_codes[r][:, g, i, :].bitcast(FP8X4),
-                    lhsT_scale=direct_scales[r][:, g, i, :],
+                    lhsT=codes[i][:, g, rows].bitcast(FP8X4),
+                    lhsT_scale=scales[i][:, g, rows],
                     rhs=wy_codes[:, g, 4 * n : 4 * n + 4, :].rearrange("p l m -> p (l m)").bitcast(FP8X4),
                     rhs_scale=wy_scales[:, g, 4 * n : 4 * n + 4, :].rearrange("p l m -> p (l m)"),
                     start=(g == 0),
                     stop=(g == PASSES - 1),
                 )
             half = y[t][:, BANK * n : BANK * (n + 1)].rearrange("b (p t) -> b p t", t=4)
-            nc.vector.tensor_tensor(
-                out=half, in0=product[:].rearrange("b (t p) -> b p t", t=4), in1=half, op=ADD
-            )
+            nc.vector.tensor_tensor(out=half, in0=product[:].rearrange("b (t p) -> b p t", t=4), in1=half, op=ADD)
             if n == 1:
                 nc.sync.dma_start(out=out[:, t, :], in_=y[t][:])
 
-        def finish_half(r, n, s):
-            if n == 0:
-                res[r, s] = res_pool.tile([P, D], F32, name="res")
+        def finish_two(c, n, s):
             cols = slice(BANK * n, BANK * (n + 1))
-            bank = psum_back.tile([P, 4, P], F32, name="bank_back")
-            for q in range(4):
-                nc.tensor.transpose(bank[:, q, :], sums[r, n][:, q, P * s : P * (s + 1)], ident_f32[:])
-            nc.vector.tensor_tensor(
-                out=res[r, s][:, cols].rearrange("b (p t) -> b p t", t=4),
-                in0=bank[:].rearrange("b t p -> b p t"),
-                in1=context[:, cols].rearrange("b (p t) -> b p t", t=4),
-                op=ADD,
-            )
-            if n == 1:
-                nc.sync.dma_start(out=out[:, STARTS[r] + s, :], in_=res[r, s][:])
+            res = res_pool.tile([P, 2, BANK], F32, name="res")
+            for j in range(2):
+                bank = psum_back.tile([P, 4, P], F32, name="bank_back")
+                for q in range(4):
+                    part = sums[c, n][:, q, P * (s + j) : P * (s + j + 1)]
+                    nc.tensor.transpose(bank[:, q, :], part, ident_f32[:])
+                nc.vector.tensor_tensor(
+                    out=res[:, j, :].rearrange("b (p t) -> b p t", t=4),
+                    in0=bank[:].rearrange("b t p -> b p t"),
+                    in1=context[:, cols].rearrange("b (p t) -> b p t", t=4),
+                    op=ADD,
+                )
+            t = CHUNKS[c] + s
+            nc.sync.dma_start(out=out[:, t : t + 2, cols], in_=res[:])
 
         for t in range(CHUNK + 1):
-            transpose_step(t, nc.scalar.copy if t % 2 == 0 else nc.vector.tensor_copy)
+            x_perm[t] = order_words(nc.vector.tensor_copy, x_rows[t].bitcast(F32))
+            place_step(t, transpose_words(x_perm[t]), nc.scalar.copy)
+        order_slabs(0)
+        turn_slabs(0)
         for g in range(PASSES):
-            quantise_chunk(0, g)
-        prepare_slabs(0)
-        prepare_slabs(1)
+            quantise(0, g)
+        order_slabs(1)
+        quantise_slabs(0)
+        turn_slabs(1)
+        order_slabs(2)
         nc.scalar.copy(out=wx[:], in_=wg[:, :, ROW - 1])
         done = CHUNK + 1
+        quantised = 1
+        started = 0
+        multiplied = 0
 
-        def direct_halves(q):
-            r = (q - 2) // CHUNK
-            k = (q - 2) % CHUNK
-            if r < 0 or r >= N_ROUNDS:
-                return []
-            halves = [(r, j, n) for j in range(DIRECT[r]) for n in range(2)]
-            return halves[len(halves) * k // CHUNK : len(halves) * (k + 1) // CHUNK]
-
-        for q in range(CHUNK * N_ROUNDS + 2):
-            i = q // CHUNK
+        for q in range(QUARTERS + 2):
+            c = q // CHUNK
             k = q % CHUNK
-            steps = []
-            if i + 1 < N_ROUNDS:
-                lead = min(LEAD, FIRST_LEAD + q // 2)
-                goal = min(LAGS, STARTS[i + 1] + -(-SIZES[i + 1] * (k + 1) // CHUNK) + lead)
-                steps = list(range(done, min(goal, done + MOST)))
-            elif done < LAGS:
-                steps = list(range(done, min(LAGS, done + MOST)))
-            done += len(steps)
-            load_steps(done + AHEAD)
-            if k == 2 and i + 1 < N_ROUNDS:
-                for j in range(DIRECT[i + 1]):
-                    start_direct(i + 1, j)
-            if i > 0:
-                for t in steps:
-                    order_words(t, nc.scalar.copy)
-            if i < N_ROUNDS:
-                multiply_slab(i, 2 * k)
-                multiply_slab(i, 2 * k + 1)
-            if 0 < i < N_ROUNDS and k < 2:
-                quantise_direct(i, k)
-            if i + 1 < N_ROUNDS and k >= 2:
-                quantise_chunk(i + 1, k - 2)
-            for r, j, n in direct_halves(q):
-                multiply_direct(r, j, n)
-            if q < 2:
-                prepare_slabs(q + 2)
-            if q == 0:
-                make_wx()
-                make_context()
-                for j in range(DIRECT[0]):
-                    start_direct(0, j)
-            if q >= 2:
-                r = (q - 2) // CHUNK
-                n = k // 2 ^ 1
-                for s in range(2 * (k % 2), 2 * (k % 2) + 2):
-                    finish_half(r, n, s)
+            goal = min(5 + 5 * (q + 1) // 2, 20 + 2 * (q - 5) if q > 5 else LAGS)
+            steps = list(range(done, min(LAGS, goal)))
+            load_steps((steps[-1] if steps else done) + AHEAD)
             for t in steps:
-                transpose_step(t, nc.vector.tensor_copy if i == 0 and t % 2 == 1 else nc.scalar.copy)
+                x_perm[t] = order_words(nc.scalar.copy, x_rows[t].bitcast(F32))
+            if q < QUARTERS:
+                multiply_slab(c, 2 * k)
+                multiply_slab(c, 2 * k + 1)
+            if q < 3:
+                quantise_slabs(q + 1)
+            if q < 2:
+                turn_slabs(q + 2)
+            if q == 0:
+                order_slabs(3)
+                make_wx()
+                turn_context()
             if q == 1:
+                make_context()
+            if quantised < len(GROUPS) and FIRST[quantised] + GROUPS[quantised][1] <= done:
                 for g in range(PASSES):
-                    quantise_direct(0, g)
+                    quantise(quantised, g)
+                quantised += 1
+            if q >= 1:
+                while started < len(DIRECT) and started < multiplied // 2 + 5 and DIRECT[started] + 1 in x_rows:
+                    start_direct(DIRECT[started])
+                    started += 1
+            due = 2 * len(DIRECT) * (q + 1 - B_FROM) // (B_TO - B_FROM) if q >= B_FROM else 0
+            while multiplied < due:
+                multiply_direct(DIRECT[multiplied // 2], multiplied % 2)
+                multiplied += 1
+            if q >= 2:
+                finish_two((q - 2) // CHUNK, k // 2 ^ 1, 2 * (k % 2))
+            for t in steps:
+                place_step(t, transpose_words(x_perm[t]), nc.scalar.copy)
+            done += len(steps)

@@ -28,11 +28,38 @@ GROUP_OF = [i for i, (_, n) in enumerate(GROUPS) for _ in range(n)]
 CHUNKS = [FIRST[i] + CHUNK * c for i, (kind, n) in enumerate(GROUPS) if kind == "C" for c in range(n // CHUNK)]
 DIRECT = [t for t in range(LAGS) if GROUPS[GROUP_OF[t]][0] == "B"]
 QUARTERS = CHUNK * len(CHUNKS)
-G_COLS = 256
+
+
+def direct_due(q):
+    return max(0, min(2 * len(DIRECT), -(-2 * len(DIRECT) * (q + 1 - B_FROM) // (B_TO - B_FROM))))
+
+
+def first_use(i):
+    if GROUPS[i][0] == "C":
+        return CHUNK * CHUNKS.index(FIRST[i])
+    j = 2 * DIRECT.index(FIRST[i])
+    return min(q for q in range(B_FROM, B_TO) if direct_due(q) > j)
+
+
+def turned_by(q):
+    most = CHUNK + 1
+    for i in range(len(GROUPS)):
+        last = FIRST[i] + GROUPS[i][1]
+        by = first_use(i) - LEAD
+        if q >= by:
+            most = max(most, last)
+        else:
+            most = max(most, CHUNK + 1 - (-(last - CHUNK - 1) * (q + 1) // (by + 1)))
+    return most
+
+
+TURNED = [t for j, t in enumerate(DIRECT) if t < 39]
+G_COLS = 1024
 AHEAD = 5
 B_FROM = 5
 B_TO = QUARTERS + 2
 WARM = 8
+LEAD = 3
 
 FLOPS = 2 * P * LAGS * D * D + 2 * P * P * D
 
@@ -161,6 +188,7 @@ def tile_npchangetransitionprior_pa_t_kernel(tc, x, emb, Wg, bg, out):
 
         wx = const.tile([P, SLABS], F32, name="wx")
         wx_all = const.tile([P, D], F32, name="wx_all")
+        wx_diag = const.tile([P, SLABS, P], BF16, name="wx_diag")
         context = const.tile([P, D], F32, name="context")
 
         def make_wx():
@@ -225,7 +253,23 @@ def tile_npchangetransitionprior_pa_t_kernel(tc, x, emb, Wg, bg, out):
 
         def start_direct(t):
             y[t] = y_pool.tile([P, D], F32, name="y")
-            for c in range(0, D, G_COLS):
+            if t in TURNED:
+                i = GROUP_OF[t + 1]
+                for n in range(PASSES):
+                    bank = psum_back.tile([P, 4, P], F32, name="bank_diag", tag="bank_back")
+                    for v in range(4):
+                        nc.tensor.matmul(
+                            bank[:, v, :],
+                            lhsT=grouped[i][:, n, t + 1 - FIRST[i], :, v],
+                            rhs=wx_diag[:, 4 * n + v, :],
+                            start=True,
+                            stop=True,
+                        )
+                    nc.scalar.copy(
+                        out=y[t][:, BANK * n : BANK * (n + 1)].rearrange("b (p t) -> b p t", t=4),
+                        in_=bank[:].rearrange("b t p -> b p t"),
+                    )
+            for c in range(0, 0 if t in TURNED else D, G_COLS):
                 cols = slice(c, c + G_COLS)
                 nc.gpsimd.tensor_tensor(out=y[t][:, cols], in0=x_rows[t + 1][:, cols], in1=wx_all[:, cols], op=MULT)
             for c in range(0, D, G_COLS):
@@ -280,6 +324,10 @@ def tile_npchangetransitionprior_pa_t_kernel(tc, x, emb, Wg, bg, out):
         turn_slabs(1)
         order_slabs(2)
         nc.scalar.copy(out=wx[:], in_=wg[:, :, ROW - 1])
+        for slab in range(SLABS):
+            nc.vector.tensor_scalar(
+                out=wx_diag[:, slab, :], in0=ident_bf16[:], scalar1=wx[:, slab : slab + 1], scalar2=None, op0=MULT
+            )
         done = CHUNK + 1
         quantised = 1
         started = 0
@@ -288,7 +336,7 @@ def tile_npchangetransitionprior_pa_t_kernel(tc, x, emb, Wg, bg, out):
         for q in range(QUARTERS + 2):
             c = q // CHUNK
             k = q % CHUNK
-            goal = min(5 + 5 * (q + 1) // 2, 20 + 2 * (q - 5) if q > 5 else LAGS)
+            goal = turned_by(q)
             steps = list(range(done, min(LAGS, goal)))
             load_steps((steps[-1] if steps else done) + AHEAD)
             for t in steps:
@@ -312,9 +360,11 @@ def tile_npchangetransitionprior_pa_t_kernel(tc, x, emb, Wg, bg, out):
                 quantised += 1
             if q >= 1:
                 while started < len(DIRECT) and started < multiplied // 2 + 5 and DIRECT[started] + 1 in x_rows:
+                    if DIRECT[started] in TURNED and (DIRECT[started] + 1 >= done or started > multiplied // 2 + 3):
+                        break
                     start_direct(DIRECT[started])
                     started += 1
-            due = 2 * len(DIRECT) * (q + 1 - B_FROM) // (B_TO - B_FROM) if q >= B_FROM else 0
+            due = direct_due(q)
             while multiplied < due:
                 multiply_direct(DIRECT[multiplied // 2], multiplied % 2)
                 multiplied += 1

@@ -22,7 +22,7 @@ WORD_BLOCKS = 4
 SLABS = 8
 CHUNK = 4
 BANK = 512
-GROUPS = [("C", 4), ("C", 4), ("B", 4), ("C", 8), ("B", 4), ("C", 8), ("B", 4), ("B", 4)]
+GROUPS = [("C", 4), ("B", 4), ("C", 4), ("B", 4), ("C", 4), ("B", 4), ("C", 4), ("B", 4), ("C", 4), ("B", 4)]
 FIRST = [sum(n for _, n in GROUPS[:i]) for i in range(len(GROUPS))]
 GROUP_OF = [i for i, (_, n) in enumerate(GROUPS) for _ in range(n)]
 CHUNKS = [FIRST[i] + CHUNK * c for i, (kind, n) in enumerate(GROUPS) if kind == "C" for c in range(n // CHUNK)]
@@ -44,7 +44,7 @@ def first_use(i):
 def turned_by(q):
     most = CHUNK + 1
     for i in range(len(GROUPS)):
-        last = FIRST[i] + GROUPS[i][1]
+        last = FIRST[i] + GROUPS[i][1] + 1
         by = first_use(i) - LEAD
         if q >= by:
             most = max(most, last)
@@ -53,13 +53,11 @@ def turned_by(q):
     return most
 
 
-TURNED = [t for j, t in enumerate(DIRECT) if t < 39]
-G_COLS = 1024
 AHEAD = 5
-B_FROM = 5
+B_FROM = 3
 B_TO = QUARTERS + 2
 WARM = 8
-LEAD = 3
+LEAD = 2
 
 FLOPS = 2 * P * LAGS * D * D + 2 * P * P * D
 
@@ -74,12 +72,13 @@ def tile_npchangetransitionprior_pa_t_kernel(tc, x, emb, Wg, bg, out):
         ctx.enter_context(tc.manual_schedule())
         const = ctx.enter_context(tc.tile_pool(name="const", bufs=1))
         rows_pool = ctx.enter_context(tc.tile_pool(name="rows_pool", bufs=9))
-        perm_pool = ctx.enter_context(tc.tile_pool(name="perm_pool", bufs=5))
-        xg_pool = ctx.enter_context(tc.tile_pool(name="xg_pool", bufs=2))
+        perm_pool = ctx.enter_context(tc.tile_pool(name="perm_pool", bufs=6))
+        xg_pool = ctx.enter_context(tc.tile_pool(name="xg_pool", bufs=3))
         xq_pool = ctx.enter_context(tc.tile_pool(name="xq_pool", bufs=2))
         wyg_pool = ctx.enter_context(tc.tile_pool(name="wyg_pool", bufs=2))
         sum_pool = ctx.enter_context(tc.tile_pool(name="sum_pool", bufs=2))
         res_pool = ctx.enter_context(tc.tile_pool(name="res_pool", bufs=3))
+        tx_pool = ctx.enter_context(tc.tile_pool(name="tx_pool", bufs=4))
         y_pool = ctx.enter_context(tc.tile_pool(name="y_pool", bufs=6))
         psum_in = ctx.enter_context(tc.psum_pool(name="psum_in", bufs=2))
         psum_mx = ctx.enter_context(tc.psum_pool(name="psum_mx", bufs=3))
@@ -92,6 +91,7 @@ def tile_npchangetransitionprior_pa_t_kernel(tc, x, emb, Wg, bg, out):
         scales = {}
         sums = {}
         y = {}
+        turned_x = {}
 
         def load_steps(until):
             while len(x_rows) <= min(until, STEPS - 1):
@@ -115,11 +115,15 @@ def tile_npchangetransitionprior_pa_t_kernel(tc, x, emb, Wg, bg, out):
         load_steps(11)
         ones = const.tile([P, P], BF16, name="ones")
         nc.vector.memset(ones[:], 1.0)
-        bias_row = const.tile([P, D], BF16, name="bias_row")
-        nc.vector.memset(bias_row[:], 0.0)
+        scratch = const.tile([P, 1], BF16, name="scratch")
+        nc.scalar.copy(out=scratch[:], in_=ones[:, 0:1])
+        zeros = const.tile([P, BANK], BF16, name="zeros")
+        nc.vector.memset(zeros[:], 0.0)
         for i in range(WARM):
             warm = psum_mx.tile([P, BANK], F32, name="warm", tag="product")
-            nc.tensor.matmul(warm[:], lhsT=ones[:], rhs=bias_row[:, 0:BANK], start=True, stop=True)
+            nc.tensor.matmul(warm[:], lhsT=ones[:], rhs=zeros[:], start=True, stop=True)
+        bias_row = const.tile([P, D], BF16, name="bias_row")
+        nc.vector.memset(bias_row[:], 0.0)
         nc.scalar.dma_start(out=bias_row[0:1, :], in_=bg.rearrange("(o d) -> o d", o=1))
         ident_f32 = const.tile([P, P], F32, name="ident_f32")
         make_identity(nc, ident_f32[:])
@@ -138,16 +142,23 @@ def tile_npchangetransitionprior_pa_t_kernel(tc, x, emb, Wg, bg, out):
             return bank
 
         def place_step(t, bank, copy):
-            i = GROUP_OF[t]
-            kind, n = GROUPS[i]
-            if t == FIRST[i]:
+            i = GROUP_OF[t] if t < LAGS else len(GROUPS)
+            kind, n = GROUPS[i] if t < LAGS else ("", 0)
+            if t < LAGS and t == FIRST[i]:
                 slots = n + 1 if kind == "C" else n
                 grouped[i] = xg_pool.tile(
                     [P, PASSES, slots, P, 4], BF16, name="grouped", tag="grouped_" + kind, align_bytes=64
                 )
                 if i > 0 and GROUPS[i - 1][0] == "C":
                     regroup(copy, bank[:], grouped[i - 1][:, :, GROUPS[i - 1][1], :, :])
-            regroup(copy, bank[:], grouped[i][:, :, t - FIRST[i], :, :])
+            if t < LAGS:
+                regroup(copy, bank[:], grouped[i][:, :, t - FIRST[i], :, :])
+            if t - 1 in DIRECT:
+                turned_x[t] = tx_pool.tile([P, SLABS, P], BF16, name="turned_x")
+                nc.scalar.copy(
+                    out=turned_x[t][:].rearrange("p (w e) b -> p w e b", e=2),
+                    in_=bank[:].bitcast(BF16).rearrange("p w (b e) -> p w e b", e=2),
+                )
 
         def quantise(i, g):
             kind, n = GROUPS[i]
@@ -187,20 +198,8 @@ def tile_npchangetransitionprior_pa_t_kernel(tc, x, emb, Wg, bg, out):
                 )
 
         wx = const.tile([P, SLABS], F32, name="wx")
-        wx_all = const.tile([P, D], F32, name="wx_all")
         wx_diag = const.tile([P, SLABS, P], BF16, name="wx_diag")
         context = const.tile([P, D], F32, name="context")
-
-        def make_wx():
-            for g in range(PASSES):
-                bank = psum_back.tile([P, 4, P], F32, name="wx_ps", tag="bank_back")
-                for t in range(4):
-                    slab = 4 * g + t
-                    nc.tensor.transpose(bank[:, t, :], wx[:, slab : slab + 1].to_broadcast([P, P]), ident_f32[:])
-                nc.scalar.copy(
-                    out=wx_all[:, BANK * g : BANK * (g + 1)].rearrange("b (p t) -> b p t", t=4),
-                    in_=bank[:].rearrange("b t p -> b p t"),
-                )
 
         emb_t = const.tile([P, P], BF16, name="emb_t")
         we_t = const.tile([P, D], BF16, name="we_t")
@@ -253,28 +252,21 @@ def tile_npchangetransitionprior_pa_t_kernel(tc, x, emb, Wg, bg, out):
 
         def start_direct(t):
             y[t] = y_pool.tile([P, D], F32, name="y")
-            if t in TURNED:
-                i = GROUP_OF[t + 1]
-                for n in range(PASSES):
-                    bank = psum_back.tile([P, 4, P], F32, name="bank_diag", tag="bank_back")
-                    for v in range(4):
-                        nc.tensor.matmul(
-                            bank[:, v, :],
-                            lhsT=grouped[i][:, n, t + 1 - FIRST[i], :, v],
-                            rhs=wx_diag[:, 4 * n + v, :],
-                            start=True,
-                            stop=True,
-                        )
-                    nc.scalar.copy(
-                        out=y[t][:, BANK * n : BANK * (n + 1)].rearrange("b (p t) -> b p t", t=4),
-                        in_=bank[:].rearrange("b t p -> b p t"),
+            for n in range(PASSES):
+                bank = psum_back.tile([P, 4, P], F32, name="bank_diag", tag="bank_back")
+                for v in range(4):
+                    nc.tensor.matmul(
+                        bank[:, v, :],
+                        lhsT=turned_x[t + 1][:, 4 * n + v, :],
+                        rhs=wx_diag[:, 4 * n + v, :],
+                        start=True,
+                        stop=True,
                     )
-            for c in range(0, 0 if t in TURNED else D, G_COLS):
-                cols = slice(c, c + G_COLS)
-                nc.gpsimd.tensor_tensor(out=y[t][:, cols], in0=x_rows[t + 1][:, cols], in1=wx_all[:, cols], op=MULT)
-            for c in range(0, D, G_COLS):
-                cols = slice(c, c + G_COLS)
-                nc.gpsimd.tensor_tensor(out=y[t][:, cols], in0=y[t][:, cols], in1=context[:, cols], op=ADD)
+                nc.scalar.copy(
+                    out=y[t][:, BANK * n : BANK * (n + 1)].rearrange("b (p t) -> b p t", t=4),
+                    in_=bank[:].rearrange("b t p -> b p t"),
+                )
+            nc.gpsimd.tensor_tensor(out=y[t][:], in0=y[t][:], in1=context[:], op=ADD)
 
         def multiply_direct(t, n):
             i = GROUP_OF[t]
@@ -323,6 +315,7 @@ def tile_npchangetransitionprior_pa_t_kernel(tc, x, emb, Wg, bg, out):
         quantise_slabs(0)
         turn_slabs(1)
         order_slabs(2)
+        quantise_slabs(1)
         nc.scalar.copy(out=wx[:], in_=wg[:, :, ROW - 1])
         for slab in range(SLABS):
             nc.vector.tensor_scalar(
@@ -333,34 +326,38 @@ def tile_npchangetransitionprior_pa_t_kernel(tc, x, emb, Wg, bg, out):
         started = 0
         multiplied = 0
 
-        for q in range(QUARTERS + 2):
+        def order_until(goal):
+            load_steps(goal + AHEAD)
+            while len(x_perm) < goal:
+                t = len(x_perm)
+                x_perm[t] = order_words(nc.scalar.copy, x_rows[t].bitcast(F32))
+
+        order_until(turned_by(0))
+
+        for q in range(max(QUARTERS + 2, B_TO)):
             c = q // CHUNK
             k = q % CHUNK
             goal = turned_by(q)
-            steps = list(range(done, min(LAGS, goal)))
-            load_steps((steps[-1] if steps else done) + AHEAD)
-            for t in steps:
-                x_perm[t] = order_words(nc.scalar.copy, x_rows[t].bitcast(F32))
+            steps = list(range(done, min(STEPS, goal)))
             if q < QUARTERS:
                 multiply_slab(c, 2 * k)
                 multiply_slab(c, 2 * k + 1)
-            if q < 3:
-                quantise_slabs(q + 1)
             if q < 2:
                 turn_slabs(q + 2)
             if q == 0:
                 order_slabs(3)
-                make_wx()
                 turn_context()
             if q == 1:
                 make_context()
+            if q < 2:
+                quantise_slabs(q + 2)
             if quantised < len(GROUPS) and FIRST[quantised] + GROUPS[quantised][1] <= done:
                 for g in range(PASSES):
                     quantise(quantised, g)
                 quantised += 1
             if q >= 1:
-                while started < len(DIRECT) and started < multiplied // 2 + 5 and DIRECT[started] + 1 in x_rows:
-                    if DIRECT[started] in TURNED and (DIRECT[started] + 1 >= done or started > multiplied // 2 + 3):
+                while started < min(len(DIRECT), q + 3 - B_FROM) and DIRECT[started] + 1 in x_rows:
+                    if DIRECT[started] + 1 >= done:
                         break
                     start_direct(DIRECT[started])
                     started += 1
@@ -368,8 +365,9 @@ def tile_npchangetransitionprior_pa_t_kernel(tc, x, emb, Wg, bg, out):
             while multiplied < due:
                 multiply_direct(DIRECT[multiplied // 2], multiplied % 2)
                 multiplied += 1
-            if q >= 2:
+            if 2 <= q < QUARTERS + 2:
                 finish_two((q - 2) // CHUNK, k // 2 ^ 1, 2 * (k % 2))
             for t in steps:
                 place_step(t, transpose_words(x_perm[t]), nc.scalar.copy)
             done += len(steps)
+            order_until(min(STEPS, turned_by(q + 1)))

@@ -22,48 +22,34 @@ WORD_BLOCKS = 4
 SLABS = 8
 CHUNK = 4
 BANK = 512
-GROUPS = [("C", 4), ("B", 4), ("C", 4), ("B", 4), ("C", 4), ("B", 4), ("C", 4), ("B", 4), ("C", 4), ("B", 4)]
-FIRST = [sum(n for _, n in GROUPS[:i]) for i in range(len(GROUPS))]
-GROUP_OF = [i for i, (_, n) in enumerate(GROUPS) for _ in range(n)]
-CHUNKS = [FIRST[i] + CHUNK * c for i, (kind, n) in enumerate(GROUPS) if kind == "C" for c in range(n // CHUNK)]
-DIRECT = [t for t in range(LAGS) if GROUPS[GROUP_OF[t]][0] == "B"]
-QUARTERS = CHUNK * len(CHUNKS)
+GROUP = 2 * CHUNK
+N_GROUPS = LAGS // GROUP
+QUARTERS = CHUNK * N_GROUPS
+DIRECT = [t for t in range(LAGS) if t % GROUP >= CHUNK]
+SPLIT = 9
+AHEAD = 5
+B_FROM = 3
+B_TO = QUARTERS + 2
+WARM = 8
 
 
 def direct_due(q):
     return max(0, min(2 * len(DIRECT), -(-2 * len(DIRECT) * (q + 1 - B_FROM) // (B_TO - B_FROM))))
 
 
-def first_use(i):
-    if GROUPS[i][0] == "C":
-        return CHUNK * CHUNKS.index(FIRST[i])
-    j = 2 * DIRECT.index(FIRST[i])
-    return min(q for q in range(B_FROM, B_TO) if direct_due(q) > j)
-
-
 def turned_by(q):
-    most = CHUNK + 1
-    for i in range(len(GROUPS)):
-        last = FIRST[i] + GROUPS[i][1] + 1
-        by = first_use(i) - LEAD
-        if q >= by:
-            most = max(most, last)
-        else:
-            most = max(most, CHUNK + 1 - (-(last - CHUNK - 1) * (q + 1) // (by + 1)))
-    return most
+    return min(5 + 5 * (q + 1) // 2, 8 + 2 * q)
 
-
-AHEAD = 5
-B_FROM = 3
-B_TO = QUARTERS + 2
-WARM = 8
-LEAD = 2
 
 FLOPS = 2 * P * LAGS * D * D + 2 * P * P * D
 
 
 def regroup(copy, bank, grouped):
     copy(out=grouped.bitcast(F32), in_=bank.rearrange("p (g u) c -> p g c u", u=2))
+
+
+def regroup_pass(copy, bank, grouped):
+    copy(out=grouped.bitcast(F32), in_=bank.rearrange("p u c -> p c u"))
 
 
 def tile_npchangetransitionprior_pa_t_kernel(tc, x, emb, Wg, bg, out):
@@ -142,34 +128,33 @@ def tile_npchangetransitionprior_pa_t_kernel(tc, x, emb, Wg, bg, out):
             return bank
 
         def place_step(t, bank, copy):
-            i = GROUP_OF[t] if t < LAGS else len(GROUPS)
-            kind, n = GROUPS[i] if t < LAGS else ("", 0)
-            if t < LAGS and t == FIRST[i]:
-                slots = n + 1 if kind == "C" else n
-                grouped[i] = xg_pool.tile(
-                    [P, PASSES, slots, P, 4], BF16, name="grouped", tag="grouped_" + kind, align_bytes=64
-                )
-                if i > 0 and GROUPS[i - 1][0] == "C":
-                    regroup(copy, bank[:], grouped[i - 1][:, :, GROUPS[i - 1][1], :, :])
             if t < LAGS:
-                regroup(copy, bank[:], grouped[i][:, :, t - FIRST[i], :, :])
-            if t - 1 in DIRECT:
+                i = t // GROUP
+                if t % GROUP == 0:
+                    for g in range(PASSES):
+                        grouped[i, g] = xg_pool.tile(
+                            [P, GROUP, P, 4], BF16, name="grouped", tag="grouped_%d" % g, align_bytes=64
+                        )
+                for g in range(PASSES):
+                    regroup_pass(copy, bank[:, 2 * g : 2 * g + 2, :], grouped[i, g][:, t % GROUP, :, :])
+            if t - 1 in DIRECT and t == LAGS:
                 turned_x[t] = tx_pool.tile([P, SLABS, P], BF16, name="turned_x")
                 nc.scalar.copy(
                     out=turned_x[t][:].rearrange("p (w e) b -> p w e b", e=2),
                     in_=bank[:].bitcast(BF16).rearrange("p w (b e) -> p w e b", e=2),
                 )
 
-        def quantise(i, g):
-            kind, n = GROUPS[i]
-            if g == 0:
-                codes[i] = xq_pool.tile([P, PASSES, n * P], U32, name="codes", tag="codes_" + kind, align_bytes=64)
-                scales[i] = xq_pool.tile([P, PASSES, n * P], U8, name="scales", tag="scales_" + kind, align_bytes=64)
-            nc.vector.quantize_mx(
-                out=codes[i][:, g, :].bitcast(FP8X4),
-                scales=scales[i][:, g, :],
-                in_=grouped[i][:, g, 0:n, :, :].rearrange("p s b v -> p (s b v)"),
-            )
+        def quantise(i, first, n):
+            if first == 0:
+                codes[i] = xq_pool.tile([P, PASSES, GROUP * P], U32, name="codes", align_bytes=64)
+                scales[i] = xq_pool.tile([P, PASSES, GROUP * P], U8, name="scales", align_bytes=64)
+            cols = slice(P * first, P * (first + n))
+            for g in range(PASSES):
+                nc.vector.quantize_mx(
+                    out=codes[i][:, g, cols].bitcast(FP8X4),
+                    scales=scales[i][:, g, cols],
+                    in_=grouped[i, g][:, first : first + n, :, :].rearrange("p s b v -> p (s b v)"),
+                )
 
         wg_words = wg[:].bitcast(F32)
         wy_codes = const.tile([P, PASSES, SLABS, P], U32, name="wy_codes", align_bytes=64)
@@ -225,9 +210,7 @@ def tile_npchangetransitionprior_pa_t_kernel(tc, x, emb, Wg, bg, out):
                 nc.vector.tensor_copy(out=context[:, cols], in_=context_ps[:])
 
         def multiply_slab(c, slab):
-            i = GROUP_OF[CHUNKS[c]]
-            s0 = CHUNKS[c] - FIRST[i]
-            cols = slice(P * s0, P * (s0 + CHUNK))
+            cols = slice(0, P * CHUNK)
             if slab % 4 == 0:
                 sums[c, slab // 4] = sum_pool.tile([P, 4, BANK], F32, name="sums")
             product = psum_mx.tile([P, BANK], F32, name="product")
@@ -236,14 +219,14 @@ def tile_npchangetransitionprior_pa_t_kernel(tc, x, emb, Wg, bg, out):
                     out=product[:],
                     lhsT=wy_codes[:, g, slab, :].bitcast(FP8X4),
                     lhsT_scale=wy_scales[:, g, slab, :],
-                    rhs=codes[i][:, g, cols].bitcast(FP8X4),
-                    rhs_scale=scales[i][:, g, cols],
+                    rhs=codes[c][:, g, cols].bitcast(FP8X4),
+                    rhs_scale=scales[c][:, g, cols],
                     start=(g == 0),
                     stop=(g == PASSES - 1),
                 )
             nc.vector.scalar_tensor_tensor(
                 out=sums[c, slab // 4][:, slab % 4, :].rearrange("p (s b) -> p s b", s=CHUNK),
-                in0=grouped[i][:, slab // 4, s0 + 1 : s0 + 1 + CHUNK, :, slab % 4],
+                in0=grouped[c, slab // 4][:, 1 : CHUNK + 1, :, slab % 4],
                 scalar=wx[:, slab : slab + 1],
                 in1=product[:].rearrange("p (s b) -> p s b", s=CHUNK),
                 op0=MULT,
@@ -257,7 +240,7 @@ def tile_npchangetransitionprior_pa_t_kernel(tc, x, emb, Wg, bg, out):
                 for v in range(4):
                     nc.tensor.matmul(
                         bank[:, v, :],
-                        lhsT=turned_x[t + 1][:, 4 * n + v, :],
+                        lhsT=grouped[(t + 1) // GROUP, n][:, (t + 1) % GROUP, :, v] if t + 1 < LAGS else turned_x[t + 1][:, 4 * n + v, :],
                         rhs=wx_diag[:, 4 * n + v, :],
                         start=True,
                         stop=True,
@@ -266,11 +249,12 @@ def tile_npchangetransitionprior_pa_t_kernel(tc, x, emb, Wg, bg, out):
                     out=y[t][:, BANK * n : BANK * (n + 1)].rearrange("b (p t) -> b p t", t=4),
                     in_=bank[:].rearrange("b t p -> b p t"),
                 )
-            nc.gpsimd.tensor_tensor(out=y[t][:], in0=y[t][:], in1=context[:], op=ADD)
+            add = nc.gpsimd.tensor_tensor
+            add(out=y[t][:], in0=y[t][:], in1=context[:], op=ADD)
 
         def multiply_direct(t, n):
-            i = GROUP_OF[t]
-            rows = slice(P * (t - FIRST[i]), P * (t - FIRST[i] + 1))
+            i = t // GROUP
+            rows = slice(P * (t % GROUP), P * (t % GROUP + 1))
             product = psum_mx.tile([P, BANK], F32, name="product")
             for g in range(PASSES):
                 nc.tensor.matmul_mx(
@@ -301,7 +285,7 @@ def tile_npchangetransitionprior_pa_t_kernel(tc, x, emb, Wg, bg, out):
                     in1=context[:, cols].rearrange("b (p t) -> b p t", t=4),
                     op=ADD,
                 )
-            t = CHUNKS[c] + s
+            t = GROUP * c + s
             nc.sync.dma_start(out=out[:, t : t + 2, cols], in_=res[:])
 
         for t in range(CHUNK + 1):
@@ -309,8 +293,7 @@ def tile_npchangetransitionprior_pa_t_kernel(tc, x, emb, Wg, bg, out):
             place_step(t, transpose_words(x_perm[t]), nc.scalar.copy)
         order_slabs(0)
         turn_slabs(0)
-        for g in range(PASSES):
-            quantise(0, g)
+        quantise(0, 0, CHUNK)
         order_slabs(1)
         quantise_slabs(0)
         turn_slabs(1)
@@ -322,17 +305,17 @@ def tile_npchangetransitionprior_pa_t_kernel(tc, x, emb, Wg, bg, out):
                 out=wx_diag[:, slab, :], in0=ident_bf16[:], scalar1=wx[:, slab : slab + 1], scalar2=None, op0=MULT
             )
         done = CHUNK + 1
-        quantised = 1
+        quantised = CHUNK
         started = 0
         multiplied = 0
 
-        def order_until(goal):
+        def order_until(goal, copy):
             load_steps(goal + AHEAD)
             while len(x_perm) < goal:
                 t = len(x_perm)
-                x_perm[t] = order_words(nc.scalar.copy, x_rows[t].bitcast(F32))
+                x_perm[t] = order_words(copy, x_rows[t].bitcast(F32))
 
-        order_until(turned_by(0))
+        order_until(turned_by(0), nc.vector.tensor_copy)
 
         for q in range(max(QUARTERS + 2, B_TO)):
             c = q // CHUNK
@@ -351,10 +334,10 @@ def tile_npchangetransitionprior_pa_t_kernel(tc, x, emb, Wg, bg, out):
                 make_context()
             if q < 2:
                 quantise_slabs(q + 2)
-            if quantised < len(GROUPS) and FIRST[quantised] + GROUPS[quantised][1] <= done:
-                for g in range(PASSES):
-                    quantise(quantised, g)
-                quantised += 1
+            whole = CHUNK if quantised % GROUP or quantised // GROUP < SPLIT else GROUP
+            if quantised < LAGS and quantised + whole <= done:
+                quantise(quantised // GROUP, quantised % GROUP, whole)
+                quantised += whole
             if q >= 1:
                 while started < min(len(DIRECT), q + 3 - B_FROM) and DIRECT[started] + 1 in x_rows:
                     if DIRECT[started] + 1 >= done:
@@ -368,6 +351,6 @@ def tile_npchangetransitionprior_pa_t_kernel(tc, x, emb, Wg, bg, out):
             if 2 <= q < QUARTERS + 2:
                 finish_two((q - 2) // CHUNK, k // 2 ^ 1, 2 * (k % 2))
             for t in steps:
-                place_step(t, transpose_words(x_perm[t]), nc.scalar.copy)
+                place_step(t, transpose_words(x_perm[t]), nc.vector.tensor_copy if False else nc.scalar.copy)
             done += len(steps)
-            order_until(min(STEPS, turned_by(q + 1)))
+            order_until(min(STEPS, turned_by(q + 1)), nc.vector.tensor_copy if q < 2 else nc.scalar.copy)

@@ -44,10 +44,6 @@ def turned_by(q):
 FLOPS = 2 * P * LAGS * D * D + 2 * P * P * D
 
 
-def regroup(copy, bank, grouped):
-    copy(out=grouped.bitcast(F32), in_=bank.rearrange("p (g u) c -> p g c u", u=2))
-
-
 def regroup_pass(copy, bank, grouped):
     copy(out=grouped.bitcast(F32), in_=bank.rearrange("p u c -> p c u"))
 
@@ -66,9 +62,9 @@ def tile_npchangetransitionprior_pa_t_kernel(tc, x, emb, Wg, bg, out):
         res_pool = ctx.enter_context(tc.tile_pool(name="res_pool", bufs=3))
         tx_pool = ctx.enter_context(tc.tile_pool(name="tx_pool", bufs=4))
         y_pool = ctx.enter_context(tc.tile_pool(name="y_pool", bufs=6))
-        psum_in = ctx.enter_context(tc.psum_pool(name="psum_in", bufs=2))
+        psum_in = ctx.enter_context(tc.psum_pool(name="psum_in", bufs=3))
         psum_mx = ctx.enter_context(tc.psum_pool(name="psum_mx", bufs=3))
-        psum_back = ctx.enter_context(tc.psum_pool(name="psum_back", bufs=3))
+        psum_back = ctx.enter_context(tc.psum_pool(name="psum_back", bufs=2))
 
         x_rows = {}
         x_perm = {}
@@ -90,13 +86,14 @@ def tile_npchangetransitionprior_pa_t_kernel(tc, x, emb, Wg, bg, out):
 
         emb_rows = const.tile([P, P], BF16, name="emb_rows")
         nc.sync.dma_start(out=emb_rows[:], in_=emb)
-        load_steps(3)
         wg = const.tile([P, SLABS, ROW_PAD], BF16, name="wg")
         wg_rows = Wg.rearrange("(g p t) c -> g p t c", p=P, t=4)
         for w in range(4):
             t = 2 * (w % 2)
             nc.sync.dma_start(out=wg[:, 2 * w : 2 * w + 2, 0:ROW], in_=wg_rows[w // 2, :, t : t + 2, :])
             if w == 0:
+                load_steps(3)
+            if w == 1:
                 load_steps(4)
         load_steps(11)
         ones = const.tile([P, P], BF16, name="ones")
@@ -137,7 +134,7 @@ def tile_npchangetransitionprior_pa_t_kernel(tc, x, emb, Wg, bg, out):
                         )
                 for g in range(PASSES):
                     regroup_pass(copy, bank[:, 2 * g : 2 * g + 2, :], grouped[i, g][:, t % GROUP, :, :])
-            if t - 1 in DIRECT and t == LAGS:
+            if t - 1 in DIRECT and (t == LAGS or t % 2 == 0):
                 turned_x[t] = tx_pool.tile([P, SLABS, P], BF16, name="turned_x")
                 nc.scalar.copy(
                     out=turned_x[t][:].rearrange("p (w e) b -> p w e b", e=2),
@@ -171,8 +168,9 @@ def tile_npchangetransitionprior_pa_t_kernel(tc, x, emb, Wg, bg, out):
             wy_grouped[w] = wyg_pool.tile([P, PASSES, 2, P, 4], BF16, name="wy_grouped", align_bytes=64)
             for e in range(2):
                 bank = transpose_words(wy_perm[2 * w + e])
-                copy = nc.vector.tensor_copy if e == 1 and w > 0 else nc.scalar.copy
-                regroup(copy, bank[:], wy_grouped[w][:, :, e, :, :])
+                copy = nc.scalar.copy
+                for g in range(PASSES):
+                    regroup_pass(copy, bank[:, 2 * g : 2 * g + 2, :], wy_grouped[w][:, g, e, :, :])
 
         def quantise_slabs(w):
             for g in range(PASSES):
@@ -236,11 +234,11 @@ def tile_npchangetransitionprior_pa_t_kernel(tc, x, emb, Wg, bg, out):
         def start_direct(t):
             y[t] = y_pool.tile([P, D], F32, name="y")
             for n in range(PASSES):
-                bank = psum_back.tile([P, 4, P], F32, name="bank_diag", tag="bank_back")
+                bank = psum_in.tile([P, 4, P], F32, name="bank_diag", tag="bank_in")
                 for v in range(4):
                     nc.tensor.matmul(
                         bank[:, v, :],
-                        lhsT=grouped[(t + 1) // GROUP, n][:, (t + 1) % GROUP, :, v] if t + 1 < LAGS else turned_x[t + 1][:, 4 * n + v, :],
+                        lhsT=turned_x[t + 1][:, 4 * n + v, :] if t + 1 in turned_x else grouped[(t + 1) // GROUP, n][:, (t + 1) % GROUP, :, v],
                         rhs=wx_diag[:, 4 * n + v, :],
                         start=True,
                         stop=True,
@@ -288,17 +286,19 @@ def tile_npchangetransitionprior_pa_t_kernel(tc, x, emb, Wg, bg, out):
             t = GROUP * c + s
             nc.sync.dma_start(out=out[:, t : t + 2, cols], in_=res[:])
 
-        for t in range(CHUNK + 1):
-            x_perm[t] = order_words(nc.vector.tensor_copy, x_rows[t].bitcast(F32))
-            place_step(t, transpose_words(x_perm[t]), nc.scalar.copy)
         order_slabs(0)
-        turn_slabs(0)
-        quantise(0, 0, CHUNK)
-        order_slabs(1)
+        for t in range(CHUNK):
+            x_perm[t] = order_words(nc.vector.tensor_copy, x_rows[t].bitcast(F32))
+            if t == 1:
+                turn_slabs(0)
+            if t > 0:
+                place_step(t - 1, transpose_words(x_perm[t - 1]), nc.scalar.copy)
+        place_step(CHUNK - 1, transpose_words(x_perm[CHUNK - 1]), nc.scalar.copy)
         quantise_slabs(0)
-        turn_slabs(1)
-        order_slabs(2)
-        quantise_slabs(1)
+        order_slabs(1)
+        x_perm[CHUNK] = order_words(nc.vector.tensor_copy, x_rows[CHUNK].bitcast(F32))
+        quantise(0, 0, CHUNK)
+        place_step(CHUNK, transpose_words(x_perm[CHUNK]), nc.scalar.copy)
         nc.scalar.copy(out=wx[:], in_=wg[:, :, ROW - 1])
         for slab in range(SLABS):
             nc.vector.tensor_scalar(
@@ -325,15 +325,18 @@ def tile_npchangetransitionprior_pa_t_kernel(tc, x, emb, Wg, bg, out):
             if q < QUARTERS:
                 multiply_slab(c, 2 * k)
                 multiply_slab(c, 2 * k + 1)
-            if q < 2:
-                turn_slabs(q + 2)
             if q == 0:
+                turn_slabs(1)
+                order_slabs(2)
+                quantise_slabs(1)
+                turn_slabs(2)
                 order_slabs(3)
                 turn_context()
+                quantise_slabs(2)
             if q == 1:
+                turn_slabs(3)
                 make_context()
-            if q < 2:
-                quantise_slabs(q + 2)
+                quantise_slabs(3)
             whole = CHUNK if quantised % GROUP or quantised // GROUP < SPLIT else GROUP
             if quantised < LAGS and quantised + whole <= done:
                 quantise(quantised // GROUP, quantised % GROUP, whole)
@@ -351,6 +354,6 @@ def tile_npchangetransitionprior_pa_t_kernel(tc, x, emb, Wg, bg, out):
             if 2 <= q < QUARTERS + 2:
                 finish_two((q - 2) // CHUNK, k // 2 ^ 1, 2 * (k % 2))
             for t in steps:
-                place_step(t, transpose_words(x_perm[t]), nc.vector.tensor_copy if False else nc.scalar.copy)
+                place_step(t, transpose_words(x_perm[t]), nc.scalar.copy)
             done += len(steps)
             order_until(min(STEPS, turned_by(q + 1)), nc.vector.tensor_copy if q < 2 else nc.scalar.copy)

@@ -154,6 +154,7 @@ def tile_npchangetransitionprior_pa_t_kernel(tc, x, emb, Wg, bg, out):
                 )
 
         wg_words = wg[:].bitcast(F32)
+        wx = const.tile([P, SLABS], F32, name="wx")
         wy_codes = const.tile([P, PASSES, SLABS, P], U32, name="wy_codes", align_bytes=64)
         wy_scales = const.tile([P, PASSES, SLABS, P], U8, name="wy_scales", align_bytes=64)
         wy_perm = {}
@@ -163,6 +164,10 @@ def tile_npchangetransitionprior_pa_t_kernel(tc, x, emb, Wg, bg, out):
             for e in range(2):
                 words = wg_words[:, 2 * w + e, P // 2 : P // 2 + D // 2]
                 wy_perm[2 * w + e] = order_words(nc.vector.tensor_copy, words)
+
+        def take_wx(w):
+            both = slice(2 * w, 2 * w + 2)
+            nc.scalar.copy(out=wx[:, both], in_=wg[:, both, ROW - 1])
 
         def turn_slabs(w):
             wy_grouped[w] = wyg_pool.tile([P, PASSES, 2, P, 4], BF16, name="wy_grouped", align_bytes=64)
@@ -180,7 +185,6 @@ def tile_npchangetransitionprior_pa_t_kernel(tc, x, emb, Wg, bg, out):
                     in_=wy_grouped[w][:, g, :, :, :].rearrange("p l m v -> p (l m v)"),
                 )
 
-        wx = const.tile([P, SLABS], F32, name="wx")
         wx_diag = const.tile([P, SLABS, P], BF16, name="wx_diag")
         context = const.tile([P, D], F32, name="context")
 
@@ -272,11 +276,21 @@ def tile_npchangetransitionprior_pa_t_kernel(tc, x, emb, Wg, bg, out):
         def finish_two(c, n, s):
             cols = slice(BANK * n, BANK * (n + 1))
             res = res_pool.tile([P, 2, BANK], F32, name="res")
+            on_scalar = False
             for j in range(2):
-                bank = psum_back.tile([P, 4, P], F32, name="bank_back")
+                if on_scalar:
+                    bank = psum_in.tile([P, 4, P], F32, name="bank_back", tag="bank_in")
+                else:
+                    bank = psum_back.tile([P, 4, P], F32, name="bank_back")
                 for q in range(4):
                     part = sums[c, n][:, q, P * (s + j) : P * (s + j + 1)]
                     nc.tensor.transpose(bank[:, q, :], part, ident_f32[:])
+                if on_scalar:
+                    nc.scalar.copy(
+                        out=res[:, j, :].rearrange("b (p t) -> b p t", t=4), in_=bank[:].rearrange("b t p -> b p t")
+                    )
+                    nc.gpsimd.tensor_tensor(out=res[:, j, :], in0=res[:, j, :], in1=context[:, cols], op=ADD)
+                    continue
                 nc.vector.tensor_tensor(
                     out=res[:, j, :].rearrange("b (p t) -> b p t", t=4),
                     in0=bank[:].rearrange("b t p -> b p t"),
@@ -299,11 +313,7 @@ def tile_npchangetransitionprior_pa_t_kernel(tc, x, emb, Wg, bg, out):
         x_perm[CHUNK] = order_words(nc.vector.tensor_copy, x_rows[CHUNK].bitcast(F32))
         quantise(0, 0, CHUNK)
         place_step(CHUNK, transpose_words(x_perm[CHUNK]), nc.scalar.copy)
-        nc.scalar.copy(out=wx[:], in_=wg[:, :, ROW - 1])
-        for slab in range(SLABS):
-            nc.vector.tensor_scalar(
-                out=wx_diag[:, slab, :], in0=ident_bf16[:], scalar1=wx[:, slab : slab + 1], scalar2=None, op0=MULT
-            )
+        take_wx(0)
         done = CHUNK + 1
         quantised = CHUNK
         started = 0
@@ -315,7 +325,6 @@ def tile_npchangetransitionprior_pa_t_kernel(tc, x, emb, Wg, bg, out):
                 t = len(x_perm)
                 x_perm[t] = order_words(copy, x_rows[t].bitcast(F32))
 
-        order_until(turned_by(0), nc.vector.tensor_copy)
 
         for q in range(max(QUARTERS + 2, B_TO)):
             c = q // CHUNK
@@ -326,11 +335,19 @@ def tile_npchangetransitionprior_pa_t_kernel(tc, x, emb, Wg, bg, out):
                 multiply_slab(c, 2 * k)
                 multiply_slab(c, 2 * k + 1)
             if q == 0:
+                order_until(turned_by(0), nc.vector.tensor_copy)
                 turn_slabs(1)
                 order_slabs(2)
                 quantise_slabs(1)
+                take_wx(1)
                 turn_slabs(2)
+                take_wx(2)
                 order_slabs(3)
+                take_wx(3)
+                for slab in range(SLABS):
+                    nc.scalar.activation(
+                        out=wx_diag[:, slab, :], in_=ident_bf16[:], func=mybir.ActivationFunctionType.Copy, scale=wx[:, slab : slab + 1]
+                    )
                 turn_context()
                 quantise_slabs(2)
             if q == 1:
@@ -347,11 +364,13 @@ def tile_npchangetransitionprior_pa_t_kernel(tc, x, emb, Wg, bg, out):
                         break
                     start_direct(DIRECT[started])
                     started += 1
+            if q >= QUARTERS:
+                finish_two((q - 2) // CHUNK, k // 2 ^ 1, 2 * (k % 2))
             due = direct_due(q)
             while multiplied < due:
                 multiply_direct(DIRECT[multiplied // 2], multiplied % 2)
                 multiplied += 1
-            if 2 <= q < QUARTERS + 2:
+            if 2 <= q < QUARTERS:
                 finish_two((q - 2) // CHUNK, k // 2 ^ 1, 2 * (k % 2))
             for t in steps:
                 place_step(t, transpose_words(x_perm[t]), nc.scalar.copy)

@@ -30,7 +30,7 @@ SPLIT = 9
 AHEAD = 5
 B_FROM = 3
 B_TO = QUARTERS + 2
-WARM = 8
+WARM = 6
 
 
 def direct_due(q):
@@ -134,12 +134,9 @@ def tile_npchangetransitionprior_pa_t_kernel(tc, x, emb, Wg, bg, out):
                         )
                 for g in range(PASSES):
                     regroup_pass(copy, bank[:, 2 * g : 2 * g + 2, :], grouped[i, g][:, t % GROUP, :, :])
-            if t - 1 in DIRECT and (t == LAGS or t % 2 == 0):
-                turned_x[t] = tx_pool.tile([P, SLABS, P], BF16, name="turned_x")
-                nc.scalar.copy(
-                    out=turned_x[t][:].rearrange("p (w e) b -> p w e b", e=2),
-                    in_=bank[:].bitcast(BF16).rearrange("p w (b e) -> p w e b", e=2),
-                )
+            if t - 1 in DIRECT:
+                turned_x[t] = tx_pool.tile([P, WORD_BLOCKS, P, 2], BF16, name="turned_x")
+                nc.scalar.copy(out=turned_x[t][:].bitcast(F32).rearrange("p w b o -> p w (b o)"), in_=bank[:])
 
         def quantise(i, first, n):
             if first == 0:
@@ -242,7 +239,7 @@ def tile_npchangetransitionprior_pa_t_kernel(tc, x, emb, Wg, bg, out):
                 for v in range(4):
                     nc.tensor.matmul(
                         bank[:, v, :],
-                        lhsT=turned_x[t + 1][:, 4 * n + v, :] if t + 1 in turned_x else grouped[(t + 1) // GROUP, n][:, (t + 1) % GROUP, :, v],
+                        lhsT=turned_x[t + 1][:, 2 * n + v // 2, :, v % 2],
                         rhs=wx_diag[:, 4 * n + v, :],
                         start=True,
                         stop=True,
@@ -276,21 +273,11 @@ def tile_npchangetransitionprior_pa_t_kernel(tc, x, emb, Wg, bg, out):
         def finish_two(c, n, s):
             cols = slice(BANK * n, BANK * (n + 1))
             res = res_pool.tile([P, 2, BANK], F32, name="res")
-            on_scalar = False
             for j in range(2):
-                if on_scalar:
-                    bank = psum_in.tile([P, 4, P], F32, name="bank_back", tag="bank_in")
-                else:
-                    bank = psum_back.tile([P, 4, P], F32, name="bank_back")
+                bank = psum_back.tile([P, 4, P], F32, name="bank_back")
                 for q in range(4):
                     part = sums[c, n][:, q, P * (s + j) : P * (s + j + 1)]
                     nc.tensor.transpose(bank[:, q, :], part, ident_f32[:])
-                if on_scalar:
-                    nc.scalar.copy(
-                        out=res[:, j, :].rearrange("b (p t) -> b p t", t=4), in_=bank[:].rearrange("b t p -> b p t")
-                    )
-                    nc.gpsimd.tensor_tensor(out=res[:, j, :], in0=res[:, j, :], in1=context[:, cols], op=ADD)
-                    continue
                 nc.vector.tensor_tensor(
                     out=res[:, j, :].rearrange("b (p t) -> b p t", t=4),
                     in0=bank[:].rearrange("b t p -> b p t"),

@@ -140,8 +140,8 @@ def tile_npchangetransitionprior_pa_t_kernel(tc, x, emb, Wg, bg, out):
 
         def quantise(i, first, n):
             if first == 0:
-                codes[i] = xq_pool.tile([P, PASSES, GROUP * P], U32, name="codes", align_bytes=64)
-                scales[i] = xq_pool.tile([P, PASSES, GROUP * P], U8, name="scales", align_bytes=64)
+                codes[i] = xq_pool.tile([P, PASSES, GROUP * P], U32, name="codes", align_bytes=256)
+                scales[i] = xq_pool.tile([P, PASSES, GROUP * P], U8, name="scales", align_bytes=256)
             cols = slice(P * first, P * (first + n))
             for g in range(PASSES):
                 nc.vector.quantize_mx(
@@ -152,8 +152,8 @@ def tile_npchangetransitionprior_pa_t_kernel(tc, x, emb, Wg, bg, out):
 
         wg_words = wg[:].bitcast(F32)
         wx = const.tile([P, SLABS], F32, name="wx")
-        wy_codes = const.tile([P, PASSES, SLABS, P], U32, name="wy_codes", align_bytes=64)
-        wy_scales = const.tile([P, PASSES, SLABS, P], U8, name="wy_scales", align_bytes=64)
+        wy_codes = const.tile([P, PASSES, SLABS, P], U32, name="wy_codes", align_bytes=256)
+        wy_scales = const.tile([P, PASSES, SLABS, P], U8, name="wy_scales", align_bytes=256)
         wy_perm = {}
         wy_grouped = {}
 

from contextlib import ExitStack

import concourse.mybir as mybir
from concourse.masks import make_identity

F32 = mybir.dt.float32
BF16 = mybir.dt.bfloat16
U32 = mybir.dt.uint32
U8 = mybir.dt.uint8
FP8X4 = mybir.dt.float8_e4m3fn_x4
ADD = mybir.AluOpType.add
MULT = mybir.AluOpType.mult

P = 128
STEPS = 41
LAGS = STEPS - 1
D = 1024
ROW = P + D + 1
ROW_PAD = 1168
PASSES = 2
WORD_BLOCKS = 4
SLABS = 8
CHUNK = 4
BANK = 512
GROUP = 2 * CHUNK
N_GROUPS = LAGS // GROUP
QUARTERS = CHUNK * N_GROUPS
DIRECT = [t for t in range(LAGS) if t % GROUP >= CHUNK]
SPLIT = 9
AHEAD = 5
B_FROM = 3
B_TO = QUARTERS + 2
WARM = 6


def direct_due(q):
    return max(0, min(2 * len(DIRECT), -(-2 * len(DIRECT) * (q + 1 - B_FROM) // (B_TO - B_FROM))))


def turned_by(q):
    return min(5 + 5 * (q + 1) // 2, 8 + 2 * q)


FLOPS = 2 * P * LAGS * D * D + 2 * P * P * D


def regroup_pass(copy, bank, grouped):
    copy(out=grouped.bitcast(F32), in_=bank.rearrange("p u c -> p c u"))


def tile_npchangetransitionprior_pa_t_kernel(tc, x, emb, Wg, bg, out):
    nc = tc.nc
    with ExitStack() as ctx:
        ctx.enter_context(tc.manual_schedule())
        const = ctx.enter_context(tc.tile_pool(name="const", bufs=1))
        rows_pool = ctx.enter_context(tc.tile_pool(name="rows_pool", bufs=9))
        perm_pool = ctx.enter_context(tc.tile_pool(name="perm_pool", bufs=6))
        xg_pool = ctx.enter_context(tc.tile_pool(name="xg_pool", bufs=3))
        xq_pool = ctx.enter_context(tc.tile_pool(name="xq_pool", bufs=2))
        wyg_pool = ctx.enter_context(tc.tile_pool(name="wyg_pool", bufs=2))
        sum_pool = ctx.enter_context(tc.tile_pool(name="sum_pool", bufs=2))
        res_pool = ctx.enter_context(tc.tile_pool(name="res_pool", bufs=3))
        tx_pool = ctx.enter_context(tc.tile_pool(name="tx_pool", bufs=4))
        y_pool = ctx.enter_context(tc.tile_pool(name="y_pool", bufs=6))
        psum_in = ctx.enter_context(tc.psum_pool(name="psum_in", bufs=3))
        psum_mx = ctx.enter_context(tc.psum_pool(name="psum_mx", bufs=3))
        psum_back = ctx.enter_context(tc.psum_pool(name="psum_back", bufs=2))

        x_rows = {}
        x_perm = {}
        grouped = {}
        codes = {}
        scales = {}
        sums = {}
        y = {}
        turned_x = {}

        def load_steps(until):
            while len(x_rows) <= min(until, STEPS - 1):
                t = len(x_rows)
                n = min(2, STEPS - t)
                pair = rows_pool.tile([P, 2, D], BF16, name="rows")
                nc.sync.dma_start(out=pair[:, 0:n, :], in_=x[:, t : t + n, :])
                for s in range(n):
                    x_rows[t + s] = pair[:, s, :]

        emb_rows = const.tile([P, P], BF16, name="emb_rows")
        nc.sync.dma_start(out=emb_rows[:], in_=emb)
        wg = const.tile([P, SLABS, ROW_PAD], BF16, name="wg")
        wg_rows = Wg.rearrange("(g p t) c -> g p t c", p=P, t=4)
        for w in range(4):
            t = 2 * (w % 2)
            nc.sync.dma_start(out=wg[:, 2 * w : 2 * w + 2, 0:ROW], in_=wg_rows[w // 2, :, t : t + 2, :])
            if w == 0:
                load_steps(3)
            if w == 1:
                load_steps(4)
        load_steps(11)
        ones = const.tile([P, P], BF16, name="ones")
        nc.vector.memset(ones[:], 1.0)
        scratch = const.tile([P, 1], BF16, name="scratch")
        nc.scalar.copy(out=scratch[:], in_=ones[:, 0:1])
        zeros = const.tile([P, BANK], BF16, name="zeros")
        nc.vector.memset(zeros[:], 0.0)
        for i in range(WARM):
            warm = psum_mx.tile([P, BANK], F32, name="warm", tag="product")
            nc.tensor.matmul(warm[:], lhsT=ones[:], rhs=zeros[:], start=True, stop=True)
        bias_row = const.tile([P, D], BF16, name="bias_row")
        nc.vector.memset(bias_row[:], 0.0)
        nc.scalar.dma_start(out=bias_row[0:1, :], in_=bg.rearrange("(o d) -> o d", o=1))
        ident_f32 = const.tile([P, P], F32, name="ident_f32")
        make_identity(nc, ident_f32[:])
        ident_bf16 = const.tile([P, P], BF16, name="ident_bf16")
        make_identity(nc, ident_bf16[:])

        def order_words(copy, words):
            perm = perm_pool.tile([P, PASSES, 2, P], F32, name="perm")
            copy(out=perm[:], in_=words.rearrange("p (g m u) -> p g u m", g=PASSES, u=2))
            return perm

        def transpose_words(perm):
            bank = psum_in.tile([P, WORD_BLOCKS, P], F32, name="bank_in")
            for w in range(WORD_BLOCKS):
                nc.tensor.transpose(bank[:, w, :], perm[:, w // 2, w % 2, :], ident_f32[:])
            return bank

        def place_step(t, bank, copy):
            if t < LAGS:
                i = t // GROUP
                if t % GROUP == 0:
                    for g in range(PASSES):
                        grouped[i, g] = xg_pool.tile(
                            [P, GROUP, P, 4], BF16, name="grouped", tag="grouped_%d" % g, align_bytes=64
                        )
                for g in range(PASSES):
                    regroup_pass(copy, bank[:, 2 * g : 2 * g + 2, :], grouped[i, g][:, t % GROUP, :, :])
            if t - 1 in DIRECT:
                turned_x[t] = tx_pool.tile([P, WORD_BLOCKS, P, 2], BF16, name="turned_x")
                nc.scalar.copy(out=turned_x[t][:].bitcast(F32).rearrange("p w b o -> p w (b o)"), in_=bank[:])

        def quantise(i, first, n):
            if first == 0:
                codes[i] = xq_pool.tile([P, PASSES, GROUP * P], U32, name="codes", align_bytes=256)
                scales[i] = xq_pool.tile([P, PASSES, GROUP * P], U8, name="scales", align_bytes=256)
            cols = slice(P * first, P * (first + n))
            for g in range(PASSES):
                nc.vector.quantize_mx(
                    out=codes[i][:, g, cols].bitcast(FP8X4),
                    scales=scales[i][:, g, cols],
                    in_=grouped[i, g][:, first : first + n, :, :].rearrange("p s b v -> p (s b v)"),
                )

        wg_words = wg[:].bitcast(F32)
        wx = const.tile([P, SLABS], F32, name="wx")
        wy_codes = const.tile([P, PASSES, SLABS, P], U32, name="wy_codes", align_bytes=256)
        wy_scales = const.tile([P, PASSES, SLABS, P], U8, name="wy_scales", align_bytes=256)
        wy_perm = {}
        wy_grouped = {}

        def order_slabs(w):
            for e in range(2):
                words = wg_words[:, 2 * w + e, P // 2 : P // 2 + D // 2]
                wy_perm[2 * w + e] = order_words(nc.vector.tensor_copy, words)

        def take_wx(w):
            both = slice(2 * w, 2 * w + 2)
            nc.scalar.copy(out=wx[:, both], in_=wg[:, both, ROW - 1])

        def turn_slabs(w):
            wy_grouped[w] = wyg_pool.tile([P, PASSES, 2, P, 4], BF16, name="wy_grouped", align_bytes=64)
            for e in range(2):
                bank = transpose_words(wy_perm[2 * w + e])
                copy = nc.scalar.copy
                for g in range(PASSES):
                    regroup_pass(copy, bank[:, 2 * g : 2 * g + 2, :], wy_grouped[w][:, g, e, :, :])

        def quantise_slabs(w):
            for g in range(PASSES):
                nc.vector.quantize_mx(
                    out=wy_codes[:, g, 2 * w : 2 * w + 2, :].rearrange("p l m -> p (l m)").bitcast(FP8X4),
                    scales=wy_scales[:, g, 2 * w : 2 * w + 2, :].rearrange("p l m -> p (l m)"),
                    in_=wy_grouped[w][:, g, :, :, :].rearrange("p l m v -> p (l m v)"),
                )

        wx_diag = const.tile([P, SLABS, P], BF16, name="wx_diag")
        context = const.tile([P, D], F32, name="context")

        emb_t = const.tile([P, P], BF16, name="emb_t")
        we_t = const.tile([P, D], BF16, name="we_t")

        def turn_context():
            emb_t_ps = psum_back.tile([P, P], BF16, name="emb_t_ps", tag="bank_back")
            nc.tensor.transpose(emb_t_ps[:], emb_rows[:], ident_bf16[:])
            nc.scalar.copy(out=emb_t[:], in_=emb_t_ps[:])
            we_t_ps = psum_back.tile([P, SLABS, P], BF16, name="we_t_ps", tag="bank_back")
            for slab in range(SLABS):
                nc.tensor.transpose(we_t_ps[:, slab, :], wg[:, slab, 0:P], ident_bf16[:])
            nc.vector.tensor_copy(
                out=we_t[:].rearrange("h (g p t) -> h g p t", p=P, t=4),
                in_=we_t_ps[:].rearrange("h (g t) p -> h g p t", t=4),
            )

        def make_context():
            for n in range(D // BANK):
                cols = slice(BANK * n, BANK * (n + 1))
                context_ps = psum_back.tile([P, BANK], F32, name="context_ps", tag="bank_back")
                nc.tensor.matmul(context_ps[:], lhsT=emb_t[:], rhs=we_t[:, cols], start=True, stop=False)
                nc.tensor.matmul(context_ps[:], lhsT=ones[:], rhs=bias_row[:, cols], start=False, stop=True)
                nc.vector.tensor_copy(out=context[:, cols], in_=context_ps[:])

        def multiply_slab(c, slab):
            cols = slice(0, P * CHUNK)
            if slab % 4 == 0:
                sums[c, slab // 4] = sum_pool.tile([P, 4, BANK], F32, name="sums")
            product = psum_mx.tile([P, BANK], F32, name="product")
            for g in range(PASSES):
                nc.tensor.matmul_mx(
                    out=product[:],
                    lhsT=wy_codes[:, g, slab, :].bitcast(FP8X4),
                    lhsT_scale=wy_scales[:, g, slab, :],
                    rhs=codes[c][:, g, cols].bitcast(FP8X4),
                    rhs_scale=scales[c][:, g, cols],
                    start=(g == 0),
                    stop=(g == PASSES - 1),
                )
            nc.vector.scalar_tensor_tensor(
                out=sums[c, slab // 4][:, slab % 4, :].rearrange("p (s b) -> p s b", s=CHUNK),
                in0=grouped[c, slab // 4][:, 1 : CHUNK + 1, :, slab % 4],
                scalar=wx[:, slab : slab + 1],
                in1=product[:].rearrange("p (s b) -> p s b", s=CHUNK),
                op0=MULT,
                op1=ADD,
            )

        def start_direct(t):
            y[t] = y_pool.tile([P, D], F32, name="y")
            for n in range(PASSES):
                bank = psum_in.tile([P, 4, P], F32, name="bank_diag", tag="bank_in")
                for v in range(4):
                    nc.tensor.matmul(
                        bank[:, v, :],
                        lhsT=turned_x[t + 1][:, 2 * n + v // 2, :, v % 2],
                        rhs=wx_diag[:, 4 * n + v, :],
                        start=True,
                        stop=True,
                    )
                nc.scalar.copy(
                    out=y[t][:, BANK * n : BANK * (n + 1)].rearrange("b (p t) -> b p t", t=4),
                    in_=bank[:].rearrange("b t p -> b p t"),
                )
            add = nc.gpsimd.tensor_tensor
            add(out=y[t][:], in0=y[t][:], in1=context[:], op=ADD)

        def multiply_direct(t, n):
            i = t // GROUP
            rows = slice(P * (t % GROUP), P * (t % GROUP + 1))
            product = psum_mx.tile([P, BANK], F32, name="product")
            for g in range(PASSES):
                nc.tensor.matmul_mx(
                    out=product[:],
                    lhsT=codes[i][:, g, rows].bitcast(FP8X4),
                    lhsT_scale=scales[i][:, g, rows],
                    rhs=wy_codes[:, g, 4 * n : 4 * n + 4, :].rearrange("p l m -> p (l m)").bitcast(FP8X4),
                    rhs_scale=wy_scales[:, g, 4 * n : 4 * n + 4, :].rearrange("p l m -> p (l m)"),
                    start=(g == 0),
                    stop=(g == PASSES - 1),
                )
            half = y[t][:, BANK * n : BANK * (n + 1)].rearrange("b (p t) -> b p t", t=4)
            nc.vector.tensor_tensor(out=half, in0=product[:].rearrange("b (t p) -> b p t", t=4), in1=half, op=ADD)
            if n == 1:
                nc.sync.dma_start(out=out[:, t, :], in_=y[t][:])

        def finish_two(c, n, s):
            cols = slice(BANK * n, BANK * (n + 1))
            res = res_pool.tile([P, 2, BANK], F32, name="res")
            for j in range(2):
                bank = psum_back.tile([P, 4, P], F32, name="bank_back")
                for q in range(4):
                    part = sums[c, n][:, q, P * (s + j) : P * (s + j + 1)]
                    nc.tensor.transpose(bank[:, q, :], part, ident_f32[:])
                nc.vector.tensor_tensor(
                    out=res[:, j, :].rearrange("b (p t) -> b p t", t=4),
                    in0=bank[:].rearrange("b t p -> b p t"),
                    in1=context[:, cols].rearrange("b (p t) -> b p t", t=4),
                    op=ADD,
                )
            t = GROUP * c + s
            nc.sync.dma_start(out=out[:, t : t + 2, cols], in_=res[:])

        order_slabs(0)
        for t in range(CHUNK):
            x_perm[t] = order_words(nc.vector.tensor_copy, x_rows[t].bitcast(F32))
            if t == 1:
                turn_slabs(0)
            if t > 0:
                place_step(t - 1, transpose_words(x_perm[t - 1]), nc.scalar.copy)
        place_step(CHUNK - 1, transpose_words(x_perm[CHUNK - 1]), nc.scalar.copy)
        quantise_slabs(0)
        order_slabs(1)
        x_perm[CHUNK] = order_words(nc.vector.tensor_copy, x_rows[CHUNK].bitcast(F32))
        quantise(0, 0, CHUNK)
        place_step(CHUNK, transpose_words(x_perm[CHUNK]), nc.scalar.copy)
        take_wx(0)
        done = CHUNK + 1
        quantised = CHUNK
        started = 0
        multiplied = 0

        def order_until(goal, copy):
            load_steps(goal + AHEAD)
            while len(x_perm) < goal:
                t = len(x_perm)
                x_perm[t] = order_words(copy, x_rows[t].bitcast(F32))


        for q in range(max(QUARTERS + 2, B_TO)):
            c = q // CHUNK
            k = q % CHUNK
            goal = turned_by(q)
            steps = list(range(done, min(STEPS, goal)))
            if q < QUARTERS:
                multiply_slab(c, 2 * k)
                multiply_slab(c, 2 * k + 1)
            if q == 0:
                order_until(turned_by(0), nc.vector.tensor_copy)
                turn_slabs(1)
                order_slabs(2)
                quantise_slabs(1)
                take_wx(1)
                turn_slabs(2)
                take_wx(2)
                order_slabs(3)
                take_wx(3)
                for slab in range(SLABS):
                    nc.scalar.activation(
                        out=wx_diag[:, slab, :], in_=ident_bf16[:], func=mybir.ActivationFunctionType.Copy, scale=wx[:, slab : slab + 1]
                    )
                turn_context()
                quantise_slabs(2)
            if q == 1:
                turn_slabs(3)
                make_context()
                quantise_slabs(3)
            whole = CHUNK if quantised % GROUP or quantised // GROUP < SPLIT else GROUP
            if quantised < LAGS and quantised + whole <= done:
                quantise(quantised // GROUP, quantised % GROUP, whole)
                quantised += whole
            if q >= 1:
                while started < min(len(DIRECT), q + 3 - B_FROM) and DIRECT[started] + 1 in x_rows:
                    if DIRECT[started] + 1 >= done:
                        break
                    start_direct(DIRECT[started])
                    started += 1
            if q >= QUARTERS:
                finish_two((q - 2) // CHUNK, k // 2 ^ 1, 2 * (k % 2))
            due = direct_due(q)
            while multiplied < due:
                multiply_direct(DIRECT[multiplied // 2], multiplied % 2)
                multiplied += 1
            if 2 <= q < QUARTERS:
                finish_two((q - 2) // CHUNK, k // 2 ^ 1, 2 * (k % 2))
            for t in steps:
                place_step(t, transpose_words(x_perm[t]), nc.scalar.copy)
            done += len(steps)
            order_until(min(STEPS, turned_by(q + 1)), nc.vector.tensor_copy if q < 2 else nc.scalar.copy)
